import numpy as np
import ml_dtypes


def mxq(x, axis, fmt="e4m3"):
    dtype, down = {"e4m3": (ml_dtypes.float8_e4m3fn, 7), "e5m2": (ml_dtypes.float8_e5m2, 14)}[fmt]
    v = np.moveaxis(np.asarray(x, np.float32).astype(ml_dtypes.bfloat16).astype(np.float64), axis, -1)
    blocks = v.reshape(v.shape[:-1] + (-1, 32))
    amax = np.abs(blocks).max(-1, keepdims=True)
    byte = np.maximum(np.where(amax > 0, np.frexp(amax)[1] - 1 + 127, 0) - down, 1)
    scale = np.exp2(byte - 127.0)
    codes = (blocks / scale).astype(np.float32).astype(dtype).astype(np.float64)
    return np.moveaxis((codes * scale).reshape(v.shape), -1, axis)


WIDE = False


def mx_kscale(k):
    if not WIDE:
        return np.ones(k)
    levels = np.array([10, -10, 5, -5, 0])
    if k % 512:
        return np.exp2(np.random.permutation(np.resize(levels, k // 32))).repeat(32)
    a = np.empty((k // 512, 16))
    for p in range(k // 512):
        a[p, :8] = np.random.permutation(np.resize(levels, 8))
        for g in range(8):
            far = levels[np.abs(levels - a[p, g]) >= 10]
            a[p, g + 8] = far[np.random.randint(len(far))]
    return np.exp2(a.ravel()).repeat(32)


BF16 = ml_dtypes.bfloat16


def bf(x):
    return np.asarray(x, np.float32).astype(BF16)


def f64(x):
    return np.asarray(x).astype(np.float64)


B, T, D, DH, H, W = 1, 1024, 512, 512, 4, 512
ROPE_BASE = 10000.0
EPS = 1.1920929e-07


def rope(u):
    freqs = ROPE_BASE ** (-2.0 * np.arange(DH // 2) / DH)
    theta = np.arange(T)[:, None] * freqs[None, :]
    cos, sin = np.cos(theta), np.sin(theta)
    u1, u2 = u[..., 0::2], u[..., 1::2]
    return np.stack([u1 * cos - u2 * sin, u1 * sin + u2 * cos], axis=-1).reshape(u.shape)


def rmsnorm(u, w):
    return u * (1.0 / np.sqrt(np.mean(u * u, axis=-1, keepdims=True) + EPS)) * w


def draw0():
    s = mx_kscale(D)
    return {"x": bf(np.random.standard_normal((B, T, D)) * s),
            "wq": bf(np.random.standard_normal((H * DH, D)) / np.sqrt(D) / s),
            "wkv": bf(np.random.standard_normal((2 * DH, D)) * 2.0 / np.sqrt(D) / s),
            "q_norm_w": bf(1.0 + 0.1 * np.random.standard_normal(DH)),
            "k_norm_w": bf(1.0 + 0.1 * np.random.standard_normal(DH))}


def core(x, wq, wkv, q_norm_w, k_norm_w):
    xq = mxq(f64(x), 2, "e4m3")
    q = xq @ mxq(f64(wq), 1, "e4m3").T
    kv = xq @ mxq(f64(wkv), 1, "e4m3").T
    k, v = kv[..., :DH], kv[..., DH:]
    q = q.reshape(B, T, H, DH).transpose(0, 2, 1, 3)
    q_rot = rmsnorm(rope(q), f64(q_norm_w))
    k_rot = rmsnorm(rope(k), f64(k_norm_w))
    return q_rot, k_rot, v


def e4m3fn_bytes(y):
    return np.clip(np.asarray(y, np.float64), -448.0, 448.0).astype(np.float32).astype(ml_dtypes.float8_e4m3fn).view(np.uint8)


def e4m3fn_values(b):
    return np.asarray(b, np.uint8).view(ml_dtypes.float8_e4m3fn).astype(np.float64)


def setup_inputs():
    d = draw0()
    x0 = np.asarray(d['wq']).astype(np.float64)
    s = (np.max(np.abs(x0), axis=(0,), keepdims=True) / 448.0).astype(np.float32)
    out = {}
    for k, v in d.items():
        if k == 'wq':
            out['wq_bytes'] = e4m3fn_bytes(x0 / s.astype(np.float64))
            out['wq_scale'] = s
        else:
            out[k] = v
    return out


def reference(x, wq_bytes, wq_scale, wkv, q_norm_w, k_norm_w):
    return core(x, e4m3fn_values(wq_bytes) * wq_scale.astype(np.float64), wkv, q_norm_w, k_norm_w)

@@ -1,0 +1,349 @@
+from contextlib import ExitStack
+import math
+
+import concourse.mybir as mybir
+from concourse.masks import make_identity
+
+F32 = mybir.dt.float32
+BF16 = mybir.dt.bfloat16
+I32 = mybir.dt.int32
+U32 = mybir.dt.uint32
+U8 = mybir.dt.uint8
+FP8 = mybir.dt.float8_e4m3fn
+FP8X4 = mybir.dt.float8_e4m3fn_x4
+ALU = mybir.AluOpType
+ACT = mybir.ActivationFunctionType
+
+P = 128
+T = 1024
+D = 512
+DH = 512
+H = 4
+NT = T // P
+ROPE_BASE = 10000.0
+EPS = 1.1920929e-07
+TWO_PI = 2.0 * math.pi
+
+QB = 3
+SQ = 2
+XV = (False, False)
+WV = (False, False, False, False)
+TABV = (False, False)
+VALV = False
+
+FLOPS = 2 * T * D * (H * DH + 2 * DH)
+
+
+def tile_attention_pa_kernel(tc, x, wq_bytes, wq_scale, wkv, q_norm_w, k_norm_w, out_0, out_1, out_2):
+    nc = tc.nc
+    with ExitStack() as ctx:
+        const = ctx.enter_context(tc.tile_pool(name="const", bufs=1))
+        stage = ctx.enter_context(tc.tile_pool(name="stage", bufs=3))
+        work = ctx.enter_context(tc.tile_pool(name="work", bufs=3))
+        psum = ctx.enter_context(tc.psum_pool(name="psum", bufs=8))
+
+        def bank_tile(shape, name):
+            if name == "qb":
+                return psum.tile(shape, F32, name=name, tag="qb", bufs=QB)
+            if name == "sq":
+                return psum.tile(shape, F32, name=name, tag="sq", bufs=SQ)
+            return psum.tile(shape, F32, name=name, tag="aux", bufs=8 - QB - SQ)
+
+        xv = x.rearrange("b (r p) k -> p (b r) k", p=P)
+        wqv = wq_bytes.rearrange("(r p) k -> p r k", p=P)
+        wkvv = wkv.rearrange("(r p) k -> p r k", p=P)
+        x_sb = []
+        wkv_sb = []
+        wq_b8 = []
+        for c in range(2):
+            x_sb.append(const.tile([P, 4, D], BF16, name="x_sb%d" % c))
+            wkv_sb.append(const.tile([P, 4, D], BF16, name="wkv_sb%d" % c))
+        for c in range(H):
+            wq_b8.append(const.tile([P, 4, D], U8, name="wq_b8_%d" % c))
+        scale_row = const.tile([P, D], F32, name="scale_row")
+        nc.gpsimd.memset(scale_row[:], 0.0)
+        qgain_row = const.tile([P, DH], BF16, name="qgain_row")
+        nc.gpsimd.memset(qgain_row[:], 0.0)
+        nc.scalar.dma_start(out=qgain_row[0:1, :], in_=q_norm_w.rearrange("(o d) -> o d", o=1))
+        kgain_bf = const.tile([P, 2, 2], BF16, name="kgain_bf")
+        nc.scalar.dma_start(out=kgain_bf[:], in_=k_norm_w.rearrange("(j p e) -> p j e", j=2, e=2))
+        nc.sync.dma_start(out=x_sb[0][:], in_=xv[:, 0:4, :])
+        nc.sync.dma_start(out=scale_row[0:1, :], in_=wq_scale)
+        nc.sync.dma_start(out=wq_b8[0][:], in_=wqv[:, 0:4, :])
+        nc.sync.dma_start(out=x_sb[1][:], in_=xv[:, 4:8, :])
+        nc.sync.dma_start(out=wq_b8[1][:], in_=wqv[:, 4:8, :])
+        nc.sync.dma_start(out=wkv_sb[0][:], in_=wkvv[:, 0:4, :])
+        nc.sync.dma_start(out=wq_b8[2][:], in_=wqv[:, 8:12, :])
+        nc.sync.dma_start(out=wq_b8[3][:], in_=wqv[:, 12:16, :])
+        nc.sync.dma_start(out=wkv_sb[1][:], in_=wkvv[:, 4:8, :])
+
+        o0 = out_0.rearrange("b h (a p) d -> p (b h a) d", p=P)
+        o1 = out_1.rearrange("b (a p) d -> p (b a) d", p=P)
+        o2 = out_2.rearrange("b (a p) d -> p (b a) d", p=P)
+
+        ident = const.tile([P, P], F32, name="ident")
+        make_identity(nc, ident[:])
+        ones_sq = const.tile([P, P], F32, name="ones_sq")
+        nc.gpsimd.memset(ones_sq[:], 1.0)
+        scale_ps = bank_tile([P, D], "scale_ps")
+        nc.tensor.matmul(out=scale_ps[:], lhsT=ones_sq[:], rhs=scale_row[:], start=True, stop=True)
+        scale_sb = const.tile([P, D], F32, name="scale_sb")
+        nc.vector.tensor_copy(out=scale_sb[:], in_=scale_ps[:])
+        trow = const.tile([P, T], F32, name="trow")
+        nc.gpsimd.iota(trow[:], pattern=[[1, T]], base=0, channel_multiplier=0, allow_small_or_imprecise_dtypes=True)
+
+        one = const.tile([P, 1], F32, name="one")
+        nc.vector.memset(one[:], 1.0)
+        warm = const.tile([P, 2], F32, name="warm")
+        nc.scalar.activation(out=warm[:, 0:1], in_=one[:], func=ACT.Sin)
+        grow = const.tile([P, 256], F32, name="grow")
+        nc.vector.tensor_scalar(out=grow[:, 0:1], in0=one[:], scalar1=1.0 / TWO_PI, scalar2=None, op0=ALU.mult)
+        for level in range(4):
+            w = 4 ** level
+            for m in range(1, 4):
+                nc.vector.tensor_scalar(
+                    out=grow[:, m * w : (m + 1) * w], in0=grow[:, 0:w], scalar1=ROPE_BASE ** (-m * w / 256.0), scalar2=None,
+                    op0=ALU.mult,
+                )
+        gps = bank_tile([P, 2, P], "gps")
+        for j in range(2):
+            nc.tensor.transpose(gps[:, j, :], grow[:, P * j : P * (j + 1)], ident[:])
+        gcol = const.tile([P, 2], F32, name="gcol")
+        nc.vector.tensor_copy(out=gcol[:], in_=gps[:, :, 0])
+
+        frac = const.tile([P, 2, T], F32, name="frac")
+        afrac = const.tile([P, 2, T], F32, name="afrac")
+        sinT = const.tile([P, 2, T], F32, name="sinT")
+        cosT = const.tile([P, 2, T], F32, name="cosT")
+        for j in range(2):
+            turns = stage.tile([P, T], I32, name="turns", tag="turns", bufs=2)
+            nc.gpsimd.tensor_scalar(out=turns[:], in0=trow[:], scalar1=gcol[:, j : j + 1], scalar2=0.0, op0=ALU.mult, op1=ALU.add)
+            nc.vector.scalar_tensor_tensor(
+                out=frac[:, j, :], in0=trow[:], scalar=gcol[:, j : j + 1], in1=turns[:], op0=ALU.mult, op1=ALU.subtract
+            )
+            nc.scalar.activation(out=afrac[:, j, :], in_=frac[:, j, :], func=ACT.Abs)
+            nc.scalar.activation(out=sinT[:, j, :], in_=frac[:, j, :], func=ACT.Sin, scale=TWO_PI)
+            nc.scalar.activation(out=cosT[:, j, :], in_=afrac[:, j, :], func=ACT.Sin, scale=-TWO_PI, bias=0.5 * math.pi)
+
+        nc.scalar.activation(out=warm[:, 1:2], in_=cosT[:, 1, T - 1 : T], func=ACT.Abs_reciprocal_sqrt, scale=0.0, bias=1.0)
+
+        ones_bf = const.tile([P, P], BF16, name="ones_bf")
+        nc.gpsimd.memset(ones_bf[:], 1.0)
+        gain_ps = bank_tile([P, DH], "gain_ps")
+        nc.tensor.matmul(out=gain_ps[:], lhsT=ones_bf[:], rhs=qgain_row[:], start=True, stop=True)
+        gq = const.tile([P, 2, DH], F32, name="gq")
+        gpv = gain_ps[:].rearrange("p (i e) -> p i e", e=2)
+        gqv = gq[:, 1, :].rearrange("p (i e) -> p i e", e=2)
+        nc.vector.tensor_copy(out=gq[:, 0, :], in_=gain_ps[:])
+        nc.vector.tensor_copy(out=gqv[:, :, 0], in_=gpv[:, :, 1])
+        nc.vector.tensor_scalar(out=gqv[:, :, 1], in0=gpv[:, :, 0], scalar1=-1.0, scalar2=None, op0=ALU.mult)
+        kg = const.tile([P, 2, 3], F32, name="kg")
+        nc.vector.tensor_copy(out=kg[:, :, 0:2], in_=kgain_bf[:])
+        nc.vector.tensor_scalar(out=kg[:, :, 2], in0=kgain_bf[:, :, 0], scalar1=-1.0, scalar2=None, op0=ALU.mult)
+
+        def turn_pair(rows0, rows1):
+            bank = bank_tile([P, 2, 2, P], "tbank")
+            for rr, rows in enumerate((rows0, rows1)):
+                words = rows.bitcast(F32)
+                for u in range(2):
+                    nc.tensor.transpose(bank[:, rr, u, :], words[:, u : D // 2 : 2], ident[:])
+            return bank
+
+        def group_tile():
+            grp = stage.tile([P, 4 * 512], BF16, name="grp", tag="grp", align_bytes=64)
+            return grp, grp[:].bitcast(F32).rearrange("p (n u) -> p n u", u=2)
+
+        def exit_plain(bank, grpw, b, on_vector):
+            dst = grpw[:, 256 * b : 256 * (b + 1), :].rearrange("p (r n) u -> p r n u", r=2)
+            src = bank[:].rearrange("p r u n -> p r n u")
+            if on_vector:
+                nc.vector.tensor_copy(out=dst, in_=src)
+            else:
+                nc.scalar.copy(out=dst, in_=src)
+
+        def exit_split(bank, grpw, j):
+            dst = grpw[:, 256 * j : 256 * (j + 1), :].rearrange("p (e r i) u -> p r e i u", e=2, r=2)
+            for rr in range(2):
+                nc.scalar.copy(out=dst[:, rr], in_=bank[:, rr].rearrange("p u (i e) -> p e i u", e=2))
+
+        def quantise(grp, codes, scales):
+            nc.vector.quantize_mx(out=codes.bitcast(FP8X4), scales=scales, in_=grp[:])
+
+        xc = const.tile([P, T], U32, name="xc", align_bytes=64)
+        xs = const.tile([P, T], U8, name="xs", align_bytes=64)
+        wc = []
+        ws = []
+        for g in range(6):
+            wc.append(const.tile([P, 512], U32, name="wc%d" % g, align_bytes=64))
+            ws.append(const.tile([P, 512], U8, name="ws%d" % g, align_bytes=64))
+
+        def x_prep(c):
+            grp, grpw = group_tile()
+            for b in range(2):
+                exit_plain(turn_pair(x_sb[c][:, 2 * b, :], x_sb[c][:, 2 * b + 1, :]), grpw, b, XV[c])
+            quantise(grp, xc[:, 512 * c : 512 * (c + 1)], xs[:, 512 * c : 512 * (c + 1)])
+
+        def wq_prep(h):
+            grp, grpw = group_tile()
+            for b in range(2):
+                wide = []
+                for rr in range(2):
+                    wqf = stage.tile([P, D], BF16, name="wqf", tag="wqf", bufs=6)
+                    nc.vector.tensor_tensor(
+                        out=wqf[:], in0=wq_b8[h][:, 2 * b + rr, :].bitcast(FP8), in1=scale_sb[:], op=ALU.mult
+                    )
+                    wide.append(wqf)
+                exit_plain(turn_pair(wide[0][:], wide[1][:]), grpw, b, WV[h])
+            quantise(grp, wc[h][:], ws[h][:])
+
+        def wk_prep():
+            grp, grpw = group_tile()
+            for j in range(2):
+                exit_split(turn_pair(wkv_sb[0][:, 2 * j, :], wkv_sb[0][:, 2 * j + 1, :]), grpw, j)
+            quantise(grp, wc[4][:], ws[4][:])
+
+        def wv_prep():
+            grp, grpw = group_tile()
+            for b in range(2):
+                exit_plain(turn_pair(wkv_sb[1][:, 2 * b, :], wkv_sb[1][:, 2 * b + 1, :]), grpw, b, False)
+            quantise(grp, wc[5][:], ws[5][:])
+
+        def mx(out, lc, ls, rc, rs):
+            nc.tensor.matmul_mx(
+                out=out, lhsT=lc.bitcast(FP8X4), lhsT_scale=ls, rhs=rc.bitcast(FP8X4), rhs_scale=rs, start=True, stop=True
+            )
+
+        def x_cols(a):
+            return xc[:, P * a : P * (a + 1)], xs[:, P * a : P * (a + 1)]
+
+        def sum_squares(bank, acc):
+            junk = stage.tile([P, 512], BF16, name="junk", tag="junk", bufs=2)
+            nc.scalar.activation(out=junk[:], in_=bank[:], func=ACT.Square, accum_out=acc)
+
+        def inv_rms(ss, name):
+            inv = const.tile(list(ss.shape), F32, name=name + "_inv")
+            nc.scalar.activation(out=inv[:], in_=ss, func=ACT.Abs_reciprocal_sqrt, scale=1.0 / DH, bias=EPS)
+            return inv
+
+        def norms(a):
+            ss = work.tile([P, H + 1], F32, name="ss", tag="ss", bufs=NT)
+            inv = work.tile([P, H + 1], F32, name="inv", tag="inv", bufs=NT)
+            lc, ls = x_cols(a)
+            for g in range(H + 1):
+                bank = bank_tile([P, 512], "sq")
+                mx(bank[:], lc, ls, wc[g][:], ws[g][:])
+                sum_squares(bank, ss[:, g : g + 1])
+            nc.scalar.activation(out=inv[:], in_=ss[:], func=ACT.Abs_reciprocal_sqrt, scale=1.0 / DH, bias=EPS)
+            return inv
+
+        def k_products(th):
+            pr = []
+            for q in range(4):
+                pr.append(work.tile([P, 2, 512], F32, name="pr%d" % q, tag="pr%d" % q, bufs=1))
+            tsl = slice(512 * th, 512 * (th + 1))
+            for j in range(2):
+                ue = []
+                for e in range(2):
+                    u = bank_tile([P, 512], "ukt")
+                    csl = slice(256 * j + P * e, 256 * j + P * (e + 1))
+                    mx(u[:], wc[4][:, csl], ws[4][:, csl], xc[:, tsl], xs[:, tsl])
+                    ue.append(u)
+                for q, (e, gi, tab) in enumerate(((0, 0, cosT), (1, 2, sinT), (0, 1, sinT), (1, 1, cosT))):
+                    nc.vector.scalar_tensor_tensor(
+                        out=pr[q][:, j, :], in0=ue[e][:], scalar=kg[:, j, gi : gi + 1], in1=tab[:, j, tsl],
+                        op0=ALU.mult, op1=ALU.mult,
+                    )
+            zs = []
+            for e in range(2):
+                z = work.tile([P, 2, 512], F32, name="zk%d" % e, tag="zk%d" % e, bufs=2)
+                nc.gpsimd.tensor_tensor(out=z[:], in0=pr[2 * e][:], in1=pr[2 * e + 1][:], op=ALU.add)
+                zs.append(z)
+            return zs
+
+        def k_finish(th, pr, invs):
+            for tb in range(4):
+                a = 4 * th + tb
+                yb = bank_tile([P, 512], "ykb")
+                for j in range(2):
+                    for e in range(2):
+                        o = yb[:, 256 * j + P * e : 256 * j + P * (e + 1)]
+                        nc.tensor.transpose(o, pr[e][:, j, P * tb : P * (tb + 1)], ident[:])
+                yk = work.tile([P, DH], F32, name="yk", tag="yk", bufs=4)
+                nc.scalar.activation(
+                    out=yk[:].rearrange("p (j i e) -> p j i e", j=2, e=2),
+                    in_=yb[:].rearrange("p (j e i) -> p j i e", j=2, e=2),
+                    func=ACT.Copy, scale=invs[a][:, H : H + 1],
+                )
+                nc.sync.dma_start(out=o1[:, a, :], in_=yk[:])
+
+        def values(a):
+            bank = bank_tile([P, 512], "vb")
+            lc, ls = x_cols(a)
+            mx(bank[:], lc, ls, wc[5][:], ws[5][:])
+            vs = work.tile([P, DH], F32, name="vs", tag="vs", bufs=4)
+            if VALV:
+                nc.vector.tensor_copy(out=vs[:], in_=bank[:])
+            else:
+                nc.scalar.copy(out=vs[:], in_=bank[:])
+            nc.sync.dma_start(out=o2[:, a, :], in_=vs[:])
+
+        def q_tables(a):
+            ps = bank_tile([P, 2, 2, P], "tab_ps")
+            for r, src in enumerate((cosT, sinT)):
+                for j in range(2):
+                    nc.tensor.transpose(ps[:, r, j, :], src[:, j, P * a : P * (a + 1)], ident[:])
+            tab = work.tile([P, 2, DH], F32, name="tab", tag="tab", bufs=3)
+            nc.vector.tensor_tensor(
+                out=tab[:].rearrange("p r (i e) -> p (r i) e", e=2),
+                in0=ps[:].rearrange("p r j i -> p (r j i)").unsqueeze(2).to_broadcast([P, DH, 2]),
+                in1=gq[:].rearrange("p r (i e) -> p (r i) e", e=2),
+                op=ALU.mult,
+            )
+            return tab
+
+        def queries(a, tab, inv):
+            lc, ls = x_cols(a)
+            for h in range(H):
+                bank = bank_tile([P, 512], "qb")
+                mx(bank[:], lc, ls, wc[h][:], ws[h][:])
+                t12 = work.tile([P, 2, DH], F32, name="t12", tag="t12", bufs=4)
+                y = work.tile([P, DH], F32, name="y", tag="y", bufs=8)
+                nc.vector.scalar_tensor_tensor(
+                    out=t12[:], in0=bank[:].unsqueeze(1).to_broadcast([P, 2, DH]), scalar=inv[:, h : h + 1],
+                    in1=tab[:], op0=ALU.mult, op1=ALU.mult,
+                )
+                nc.gpsimd.tensor_tensor(
+                    out=y[:].rearrange("p (i e) -> p i e", e=2),
+                    in0=t12[:, 0, :].rearrange("p (i e) -> p i e", e=2),
+                    in1=t12[:, 1, :].rearrange("p (i e) -> p i e", e=2)[:, :, ::-1],
+                    op=ALU.add,
+                )
+                nc.sync.dma_start(out=o0[:, h * NT + a, :], in_=y[:])
+
+        x_prep(0)
+        for h in range(H):
+            wq_prep(h)
+        wk_prep()
+        invs = [norms(0)]
+        tabs = [q_tables(0)]
+        x_prep(1)
+        for a in range(NT):
+            if a + 1 < NT:
+                invs.append(norms(a + 1))
+                tabs.append(q_tables(a + 1))
+            queries(a, tabs[a], invs[a])
+            if a == 0:
+                pr0 = k_products(0)
+            elif a == 1:
+                pr1 = k_products(1)
+            elif a == 2:
+                wv_prep()
+                for v in range(4):
+                    values(v)
+            elif a == 3:
+                k_finish(0, pr0, invs)
+            elif a == 5:
+                for v in range(4, NT):
+                    values(v)
+            elif a == 6:
+                k_finish(1, pr1, invs)

@@ -62,19 +62,18 @@ def tile_attention_pa_kernel(tc, x, wq_bytes, wq_scale, wkv, q_norm_w, k_norm_w,
             wq_b8.append(const.tile([P, 4, D], U8, name="wq_b8_%d" % c))
         scale_row = const.tile([P, D], F32, name="scale_row")
         nc.gpsimd.memset(scale_row[:], 0.0)
-        qgain_row = const.tile([P, DH], BF16, name="qgain_row")
-        nc.gpsimd.memset(qgain_row[:], 0.0)
-        nc.scalar.dma_start(out=qgain_row[0:1, :], in_=q_norm_w.rearrange("(o d) -> o d", o=1))
+        gq = const.tile([P, 2, DH], BF16, name="gq")
         kgain_bf = const.tile([P, 2, 2], BF16, name="kgain_bf")
-        nc.scalar.dma_start(out=kgain_bf[:], in_=k_norm_w.rearrange("(j p e) -> p j e", j=2, e=2))
         nc.sync.dma_start(out=x_sb[0][:], in_=xv[:, 0:4, :])
         nc.sync.dma_start(out=scale_row[0:1, :], in_=wq_scale)
         nc.sync.dma_start(out=wq_b8[0][:], in_=wqv[:, 0:4, :])
-        nc.sync.dma_start(out=x_sb[1][:], in_=xv[:, 4:8, :])
         nc.sync.dma_start(out=wq_b8[1][:], in_=wqv[:, 4:8, :])
-        nc.sync.dma_start(out=wkv_sb[0][:], in_=wkvv[:, 0:4, :])
         nc.sync.dma_start(out=wq_b8[2][:], in_=wqv[:, 8:12, :])
         nc.sync.dma_start(out=wq_b8[3][:], in_=wqv[:, 12:16, :])
+        nc.sync.dma_start(out=gq[:, 0, :], in_=q_norm_w.partition_broadcast(P))
+        nc.sync.dma_start(out=kgain_bf[:], in_=k_norm_w.rearrange("(j p e) -> p j e", j=2, e=2))
+        nc.sync.dma_start(out=wkv_sb[0][:], in_=wkvv[:, 0:4, :])
+        nc.sync.dma_start(out=x_sb[1][:], in_=xv[:, 4:8, :])
         nc.sync.dma_start(out=wkv_sb[1][:], in_=wkvv[:, 4:8, :])
 
         o0 = out_0.rearrange("b h (a p) d -> p (b h a) d", p=P)
@@ -88,7 +87,7 @@ def tile_attention_pa_kernel(tc, x, wq_bytes, wq_scale, wkv, q_norm_w, k_norm_w,
         scale_ps = bank_tile([P, D], "scale_ps")
         nc.tensor.matmul(out=scale_ps[:], lhsT=ones_sq[:], rhs=scale_row[:], start=True, stop=True)
         scale_sb = const.tile([P, D], F32, name="scale_sb")
-        nc.vector.tensor_copy(out=scale_sb[:], in_=scale_ps[:])
+        nc.scalar.copy(out=scale_sb[:], in_=scale_ps[:])
         trow = const.tile([P, T], F32, name="trow")
         nc.gpsimd.iota(trow[:], pattern=[[1, T]], base=0, channel_multiplier=0, allow_small_or_imprecise_dtypes=True)
 
@@ -127,14 +126,8 @@ def tile_attention_pa_kernel(tc, x, wq_bytes, wq_scale, wkv, q_norm_w, k_norm_w,
 
         nc.scalar.activation(out=warm[:, 1:2], in_=cosT[:, 1, T - 1 : T], func=ACT.Abs_reciprocal_sqrt, scale=0.0, bias=1.0)
 
-        ones_bf = const.tile([P, P], BF16, name="ones_bf")
-        nc.gpsimd.memset(ones_bf[:], 1.0)
-        gain_ps = bank_tile([P, DH], "gain_ps")
-        nc.tensor.matmul(out=gain_ps[:], lhsT=ones_bf[:], rhs=qgain_row[:], start=True, stop=True)
-        gq = const.tile([P, 2, DH], F32, name="gq")
-        gpv = gain_ps[:].rearrange("p (i e) -> p i e", e=2)
+        gpv = gq[:, 0, :].rearrange("p (i e) -> p i e", e=2)
         gqv = gq[:, 1, :].rearrange("p (i e) -> p i e", e=2)
-        nc.vector.tensor_copy(out=gq[:, 0, :], in_=gain_ps[:])
         nc.vector.tensor_copy(out=gqv[:, :, 0], in_=gpv[:, :, 1])
         nc.vector.tensor_scalar(out=gqv[:, :, 1], in0=gpv[:, :, 0], scalar1=-1.0, scalar2=None, op0=ALU.mult)
         kg = const.tile([P, 2, 3], F32, name="kg")
@@ -226,13 +219,24 @@ def tile_attention_pa_kernel(tc, x, wq_bytes, wq_scale, wkv, q_norm_w, k_norm_w,
             return inv
 
         def norms(a):
-            ss = work.tile([P, H + 1], F32, name="ss", tag="ss", bufs=NT)
-            inv = work.tile([P, H + 1], F32, name="inv", tag="inv", bufs=NT)
+            ss = work.tile([P, H], F32, name="ss", tag="ss", bufs=NT + 2)
+            inv = work.tile([P, H], F32, name="inv", tag="inv", bufs=NT + 2)
             lc, ls = x_cols(a)
-            for g in range(H + 1):
+            for g in range(H):
                 bank = bank_tile([P, 512], "sq")
                 mx(bank[:], lc, ls, wc[g][:], ws[g][:])
                 sum_squares(bank, ss[:, g : g + 1])
+            nc.scalar.activation(out=inv[:], in_=ss[:], func=ACT.Abs_reciprocal_sqrt, scale=1.0 / DH, bias=EPS)
+            return inv
+
+        def k_norms(th):
+            ss = work.tile([P, H], F32, name="ss", tag="ss", bufs=NT + 2)
+            inv = work.tile([P, H], F32, name="inv", tag="inv", bufs=NT + 2)
+            for tb in range(4):
+                lc, ls = x_cols(4 * th + tb)
+                bank = bank_tile([P, 512], "sq")
+                mx(bank[:], lc, ls, wc[H][:], ws[H][:])
+                sum_squares(bank, ss[:, tb : tb + 1])
             nc.scalar.activation(out=inv[:], in_=ss[:], func=ACT.Abs_reciprocal_sqrt, scale=1.0 / DH, bias=EPS)
             return inv
 
@@ -260,7 +264,7 @@ def tile_attention_pa_kernel(tc, x, wq_bytes, wq_scale, wkv, q_norm_w, k_norm_w,
                 zs.append(z)
             return zs
 
-        def k_finish(th, pr, invs):
+        def k_finish(th, pr, inv):
             for tb in range(4):
                 a = 4 * th + tb
                 yb = bank_tile([P, 512], "ykb")
@@ -272,7 +276,7 @@ def tile_attention_pa_kernel(tc, x, wq_bytes, wq_scale, wkv, q_norm_w, k_norm_w,
                 nc.scalar.activation(
                     out=yk[:].rearrange("p (j i e) -> p j i e", j=2, e=2),
                     in_=yb[:].rearrange("p (j e i) -> p j i e", j=2, e=2),
-                    func=ACT.Copy, scale=invs[a][:, H : H + 1],
+                    func=ACT.Copy, scale=inv[:, tb : tb + 1],
                 )
                 nc.sync.dma_start(out=o1[:, a, :], in_=yk[:])
 
@@ -323,9 +327,9 @@ def tile_attention_pa_kernel(tc, x, wq_bytes, wq_scale, wkv, q_norm_w, k_norm_w,
         x_prep(0)
         for h in range(H):
             wq_prep(h)
-        wk_prep()
         invs = [norms(0)]
         tabs = [q_tables(0)]
+        wk_prep()
         x_prep(1)
         for a in range(NT):
             if a + 1 < NT:
@@ -336,14 +340,17 @@ def tile_attention_pa_kernel(tc, x, wq_bytes, wq_scale, wkv, q_norm_w, k_norm_w,
                 pr0 = k_products(0)
             elif a == 1:
                 pr1 = k_products(1)
+                invk0 = k_norms(0)
             elif a == 2:
                 wv_prep()
                 for v in range(4):
                     values(v)
             elif a == 3:
-                k_finish(0, pr0, invs)
+                k_finish(0, pr0, invk0)
+            elif a == 4:
+                invk1 = k_norms(1)
             elif a == 5:
                 for v in range(4, NT):
                     values(v)
             elif a == 6:
-                k_finish(1, pr1, invs)
+                k_finish(1, pr1, invk1)

@@ -26,8 +26,8 @@ TWO_PI = 2.0 * math.pi
 
 QB = 3
 SQ = 2
-XV = (False, False)
-WV = (False, False, False, False)
+XV = (True, False)
+WV = (True, False, False, False)
 TABV = (False, False)
 VALV = False
 
@@ -87,7 +87,7 @@ def tile_attention_pa_kernel(tc, x, wq_bytes, wq_scale, wkv, q_norm_w, k_norm_w,
         scale_ps = bank_tile([P, D], "scale_ps")
         nc.tensor.matmul(out=scale_ps[:], lhsT=ones_sq[:], rhs=scale_row[:], start=True, stop=True)
         scale_sb = const.tile([P, D], F32, name="scale_sb")
-        nc.scalar.copy(out=scale_sb[:], in_=scale_ps[:])
+        nc.vector.tensor_copy(out=scale_sb[:], in_=scale_ps[:])
         trow = const.tile([P, T], F32, name="trow")
         nc.gpsimd.iota(trow[:], pattern=[[1, T]], base=0, channel_multiplier=0, allow_small_or_imprecise_dtypes=True)
 

@@ -226,7 +226,12 @@ def tile_attention_pa_kernel(tc, x, wq_bytes, wq_scale, wkv, q_norm_w, k_norm_w,
                 bank = bank_tile([P, 512], "sq")
                 mx(bank[:], lc, ls, wc[g][:], ws[g][:])
                 sum_squares(bank, ss[:, g : g + 1])
-            nc.scalar.activation(out=inv[:], in_=ss[:], func=ACT.Abs_reciprocal_sqrt, scale=1.0 / DH, bias=EPS)
+                if a == 0:
+                    nc.scalar.activation(
+                        out=inv[:, g : g + 1], in_=ss[:, g : g + 1], func=ACT.Abs_reciprocal_sqrt, scale=1.0 / DH, bias=EPS
+                    )
+            if a > 0:
+                nc.scalar.activation(out=inv[:], in_=ss[:], func=ACT.Abs_reciprocal_sqrt, scale=1.0 / DH, bias=EPS)
             return inv
 
         def k_norms(th):

@@ -16,20 +16,25 @@ ACT = mybir.ActivationFunctionType
 
 P = 128
 T = 1024
+HT = T // 2
 D = 512
 DH = 512
 H = 4
 NT = T // P
+NQ = NT * H
 ROPE_BASE = 10000.0
 EPS = 1.1920929e-07
 TWO_PI = 2.0 * math.pi
 
-QB = 3
-SQ = 2
-XV = (True, False)
-WV = (True, False, False, False)
-TABV = (False, False)
-VALV = False
+VR = 4
+SR = 4
+VADD = (NQ - 1,)
+SOLO = (NQ - 2, NQ - 1)
+PRB = 2
+TABB = 4
+T12B = 3
+YB = 4
+GT0 = 4
 
 FLOPS = 2 * T * D * (H * DH + 2 * DH)
 
@@ -41,13 +46,13 @@ def tile_attention_pa_kernel(tc, x, wq_bytes, wq_scale, wkv, q_norm_w, k_norm_w,
         stage = ctx.enter_context(tc.tile_pool(name="stage", bufs=3))
         work = ctx.enter_context(tc.tile_pool(name="work", bufs=3))
         psum = ctx.enter_context(tc.psum_pool(name="psum", bufs=8))
+        ctx.enter_context(tc.manual_schedule())
 
-        def bank_tile(shape, name):
-            if name == "qb":
-                return psum.tile(shape, F32, name=name, tag="qb", bufs=QB)
-            if name == "sq":
-                return psum.tile(shape, F32, name=name, tag="sq", bufs=SQ)
-            return psum.tile(shape, F32, name=name, tag="aux", bufs=8 - QB - SQ)
+        def v_tile(shape, name):
+            return psum.tile(shape, F32, name=name, tag="vb", bufs=VR)
+
+        def s_tile(shape, name):
+            return psum.tile(shape, F32, name=name, tag="sb", bufs=SR)
 
         xv = x.rearrange("b (r p) k -> p (b r) k", p=P)
         wqv = wq_bytes.rearrange("(r p) k -> p r k", p=P)
@@ -61,35 +66,30 @@ def tile_attention_pa_kernel(tc, x, wq_bytes, wq_scale, wkv, q_norm_w, k_norm_w,
         for c in range(H):
             wq_b8.append(const.tile([P, 4, D], U8, name="wq_b8_%d" % c))
         scale_row = const.tile([P, D], F32, name="scale_row")
+        ident = const.tile([P, P], F32, name="ident")
+        trow = [const.tile([P, HT], F32, name="trow%d" % th) for th in range(2)]
+        make_identity(nc, ident[:])
         nc.gpsimd.memset(scale_row[:], 0.0)
+        nc.gpsimd.iota(trow[0][:], pattern=[[1, HT]], base=0, channel_multiplier=0, allow_small_or_imprecise_dtypes=True)
         gq = const.tile([P, 2, DH], BF16, name="gq")
         kgain_bf = const.tile([P, 2, 2], BF16, name="kgain_bf")
+        qgain_bf = const.tile([P, 2, 2], BF16, name="qgain_bf")
         nc.sync.dma_start(out=x_sb[0][:], in_=xv[:, 0:4, :])
         nc.sync.dma_start(out=scale_row[0:1, :], in_=wq_scale)
         nc.sync.dma_start(out=wq_b8[0][:], in_=wqv[:, 0:4, :])
+        nc.sync.dma_start(out=wkv_sb[0][:], in_=wkvv[:, 0:4, :])
         nc.sync.dma_start(out=wq_b8[1][:], in_=wqv[:, 4:8, :])
+        nc.sync.dma_start(out=kgain_bf[:], in_=k_norm_w.rearrange("(j p e) -> p j e", j=2, e=2))
+        nc.sync.dma_start(out=qgain_bf[:], in_=q_norm_w.rearrange("(j p e) -> p j e", j=2, e=2))
+        nc.sync.dma_start(out=gq[:, 0, :], in_=q_norm_w.partition_broadcast(P))
         nc.sync.dma_start(out=wq_b8[2][:], in_=wqv[:, 8:12, :])
         nc.sync.dma_start(out=wq_b8[3][:], in_=wqv[:, 12:16, :])
-        nc.sync.dma_start(out=gq[:, 0, :], in_=q_norm_w.partition_broadcast(P))
-        nc.sync.dma_start(out=kgain_bf[:], in_=k_norm_w.rearrange("(j p e) -> p j e", j=2, e=2))
-        nc.sync.dma_start(out=wkv_sb[0][:], in_=wkvv[:, 0:4, :])
         nc.sync.dma_start(out=x_sb[1][:], in_=xv[:, 4:8, :])
         nc.sync.dma_start(out=wkv_sb[1][:], in_=wkvv[:, 4:8, :])
 
-        o0 = out_0.rearrange("b h (a p) d -> p (b h a) d", p=P)
+        o0v = out_0.rearrange("b h (a p) d -> p (b h) a d", p=P)
         o1 = out_1.rearrange("b (a p) d -> p (b a) d", p=P)
         o2 = out_2.rearrange("b (a p) d -> p (b a) d", p=P)
-
-        ident = const.tile([P, P], F32, name="ident")
-        make_identity(nc, ident[:])
-        ones_sq = const.tile([P, P], F32, name="ones_sq")
-        nc.gpsimd.memset(ones_sq[:], 1.0)
-        scale_ps = bank_tile([P, D], "scale_ps")
-        nc.tensor.matmul(out=scale_ps[:], lhsT=ones_sq[:], rhs=scale_row[:], start=True, stop=True)
-        scale_sb = const.tile([P, D], F32, name="scale_sb")
-        nc.vector.tensor_copy(out=scale_sb[:], in_=scale_ps[:])
-        trow = const.tile([P, T], F32, name="trow")
-        nc.gpsimd.iota(trow[:], pattern=[[1, T]], base=0, channel_multiplier=0, allow_small_or_imprecise_dtypes=True)
 
         one = const.tile([P, 1], F32, name="one")
         nc.vector.memset(one[:], 1.0)
@@ -104,38 +104,47 @@ def tile_attention_pa_kernel(tc, x, wq_bytes, wq_scale, wkv, q_norm_w, k_norm_w,
                     out=grow[:, m * w : (m + 1) * w], in0=grow[:, 0:w], scalar1=ROPE_BASE ** (-m * w / 256.0), scalar2=None,
                     op0=ALU.mult,
                 )
-        gps = bank_tile([P, 2, P], "gps")
+        gps = s_tile([P, 2, P], "gps")
         for j in range(2):
             nc.tensor.transpose(gps[:, j, :], grow[:, P * j : P * (j + 1)], ident[:])
         gcol = const.tile([P, 2], F32, name="gcol")
-        nc.vector.tensor_copy(out=gcol[:], in_=gps[:, :, 0])
+        nc.scalar.copy(out=gcol[:], in_=gps[:, :, 0])
+        ones_sq = const.tile([P, P], F32, name="ones_sq")
+        nc.vector.memset(ones_sq[:], 1.0)
+        scale_sb = const.tile([P, D], F32, name="scale_sb")
 
-        frac = const.tile([P, 2, T], F32, name="frac")
-        afrac = const.tile([P, 2, T], F32, name="afrac")
-        sinT = const.tile([P, 2, T], F32, name="sinT")
-        cosT = const.tile([P, 2, T], F32, name="cosT")
-        for j in range(2):
-            turns = stage.tile([P, T], I32, name="turns", tag="turns", bufs=2)
-            nc.gpsimd.tensor_scalar(out=turns[:], in0=trow[:], scalar1=gcol[:, j : j + 1], scalar2=0.0, op0=ALU.mult, op1=ALU.add)
-            nc.vector.scalar_tensor_tensor(
-                out=frac[:, j, :], in0=trow[:], scalar=gcol[:, j : j + 1], in1=turns[:], op0=ALU.mult, op1=ALU.subtract
-            )
-            nc.scalar.activation(out=afrac[:, j, :], in_=frac[:, j, :], func=ACT.Abs)
-            nc.scalar.activation(out=sinT[:, j, :], in_=frac[:, j, :], func=ACT.Sin, scale=TWO_PI)
-            nc.scalar.activation(out=cosT[:, j, :], in_=afrac[:, j, :], func=ACT.Sin, scale=-TWO_PI, bias=0.5 * math.pi)
+        sinT = [const.tile([P, 2, HT], F32, name="sinT%d" % th) for th in range(2)]
+        cosT = [const.tile([P, 2, HT], F32, name="cosT%d" % th) for th in range(2)]
+        half = [slice(0, HT), slice(HT, T)]
+        nc.vector.tensor_scalar(out=trow[1][:], in0=trow[0][:], scalar1=float(HT), scalar2=None, op0=ALU.add)
 
-        nc.scalar.activation(out=warm[:, 1:2], in_=cosT[:, 1, T - 1 : T], func=ACT.Abs_reciprocal_sqrt, scale=0.0, bias=1.0)
+        def turns_of(th):
+            tiles = []
+            for j in range(2):
+                turns = stage.tile([P, HT], I32, name="turns", tag="turns", bufs=4)
+                nc.gpsimd.tensor_scalar(
+                    out=turns[:], in0=trow[th][:], scalar1=gcol[:, j : j + 1], scalar2=0.0, op0=ALU.mult, op1=ALU.add
+                )
+                tiles.append(turns)
+            return tiles
 
-        gpv = gq[:, 0, :].rearrange("p (i e) -> p i e", e=2)
-        gqv = gq[:, 1, :].rearrange("p (i e) -> p i e", e=2)
-        nc.vector.tensor_copy(out=gqv[:, :, 0], in_=gpv[:, :, 1])
-        nc.vector.tensor_scalar(out=gqv[:, :, 1], in0=gpv[:, :, 0], scalar1=-1.0, scalar2=None, op0=ALU.mult)
-        kg = const.tile([P, 2, 3], F32, name="kg")
-        nc.vector.tensor_copy(out=kg[:, :, 0:2], in_=kgain_bf[:])
-        nc.vector.tensor_scalar(out=kg[:, :, 2], in0=kgain_bf[:, :, 0], scalar1=-1.0, scalar2=None, op0=ALU.mult)
+        def fractions(th, turns):
+            frac = stage.tile([P, 2, HT], F32, name="frac", tag="frac", bufs=2)
+            for j in range(2):
+                nc.vector.scalar_tensor_tensor(
+                    out=frac[:, j, :], in0=trow[th][:], scalar=gcol[:, j : j + 1], in1=turns[j][:],
+                    op0=ALU.mult, op1=ALU.subtract,
+                )
+            return frac
 
-        def turn_pair(rows0, rows1):
-            bank = bank_tile([P, 2, 2, P], "tbank")
+        def sin_cos(th, frac):
+            afrac = stage.tile([P, 2, HT], F32, name="afrac", tag="afrac", bufs=1)
+            nc.scalar.activation(out=afrac[:], in_=frac[:], func=ACT.Abs)
+            nc.scalar.activation(out=sinT[th][:], in_=frac[:], func=ACT.Sin, scale=TWO_PI)
+            nc.scalar.activation(out=cosT[th][:], in_=afrac[:], func=ACT.Sin, scale=-TWO_PI, bias=0.5 * math.pi)
+
+        def turn_pair(rows0, rows1, on_vector=False):
+            bank = (v_tile if on_vector else s_tile)([P, 2, 2, P], "tbank")
             for rr, rows in enumerate((rows0, rows1)):
                 words = rows.bitcast(F32)
                 for u in range(2):
@@ -170,37 +179,6 @@ def tile_attention_pa_kernel(tc, x, wq_bytes, wq_scale, wkv, q_norm_w, k_norm_w,
             wc.append(const.tile([P, 512], U32, name="wc%d" % g, align_bytes=64))
             ws.append(const.tile([P, 512], U8, name="ws%d" % g, align_bytes=64))
 
-        def x_prep(c):
-            grp, grpw = group_tile()
-            for b in range(2):
-                exit_plain(turn_pair(x_sb[c][:, 2 * b, :], x_sb[c][:, 2 * b + 1, :]), grpw, b, XV[c])
-            quantise(grp, xc[:, 512 * c : 512 * (c + 1)], xs[:, 512 * c : 512 * (c + 1)])
-
-        def wq_prep(h):
-            grp, grpw = group_tile()
-            for b in range(2):
-                wide = []
-                for rr in range(2):
-                    wqf = stage.tile([P, D], BF16, name="wqf", tag="wqf", bufs=6)
-                    nc.vector.tensor_tensor(
-                        out=wqf[:], in0=wq_b8[h][:, 2 * b + rr, :].bitcast(FP8), in1=scale_sb[:], op=ALU.mult
-                    )
-                    wide.append(wqf)
-                exit_plain(turn_pair(wide[0][:], wide[1][:]), grpw, b, WV[h])
-            quantise(grp, wc[h][:], ws[h][:])
-
-        def wk_prep():
-            grp, grpw = group_tile()
-            for j in range(2):
-                exit_split(turn_pair(wkv_sb[0][:, 2 * j, :], wkv_sb[0][:, 2 * j + 1, :]), grpw, j)
-            quantise(grp, wc[4][:], ws[4][:])
-
-        def wv_prep():
-            grp, grpw = group_tile()
-            for b in range(2):
-                exit_plain(turn_pair(wkv_sb[1][:, 2 * b, :], wkv_sb[1][:, 2 * b + 1, :]), grpw, b, False)
-            quantise(grp, wc[5][:], ws[5][:])
-
         def mx(out, lc, ls, rc, rs):
             nc.tensor.matmul_mx(
                 out=out, lhsT=lc.bitcast(FP8X4), lhsT_scale=ls, rhs=rc.bitcast(FP8X4), rhs_scale=rs, start=True, stop=True
@@ -209,99 +187,133 @@ def tile_attention_pa_kernel(tc, x, wq_bytes, wq_scale, wkv, q_norm_w, k_norm_w,
         def x_cols(a):
             return xc[:, P * a : P * (a + 1)], xs[:, P * a : P * (a + 1)]
 
-        def sum_squares(bank, acc):
+        def x_turn(c, on_vector):
+            grp, grpw = group_tile()
+            banks = [turn_pair(x_sb[c][:, 2 * b, :], x_sb[c][:, 2 * b + 1, :], on_vector) for b in range(2)]
+            for b in range(2):
+                exit_plain(banks[b], grpw, b, on_vector)
+            return grp
+
+        def x_quant(c, grp):
+            quantise(grp, xc[:, 512 * c : 512 * (c + 1)], xs[:, 512 * c : 512 * (c + 1)])
+
+        def widen(h, b):
+            wide = []
+            for rr in range(2):
+                wqf = stage.tile([P, D], BF16, name="wqf", tag="wqf", bufs=8)
+                nc.vector.tensor_tensor(out=wqf[:], in0=wq_b8[h][:, 2 * b + rr, :].bitcast(FP8), in1=scale_sb[:], op=ALU.mult)
+                wide.append(wqf)
+            return wide
+
+        def wkv_turn(c):
+            return [turn_pair(wkv_sb[c][:, 2 * b, :], wkv_sb[c][:, 2 * b + 1, :]) for b in range(2)]
+
+        ssq = []
+        inv = []
+        for a in range(NT):
+            ssq.append(const.tile([P, H], F32, name="ssq%d" % a))
+            inv.append(const.tile([P, H], F32, name="inv%d" % a))
+        ssk = const.tile([P, NT], F32, name="ssk")
+        invk = const.tile([P, NT], F32, name="invk")
+
+        def square_bank(a, g):
+            bank = s_tile([P, 512], "sq")
+            lc, ls = x_cols(a)
+            mx(bank[:], lc, ls, wc[g][:], ws[g][:])
+            return bank
+
+        def square(bank, acc):
             junk = stage.tile([P, 512], BF16, name="junk", tag="junk", bufs=2)
             nc.scalar.activation(out=junk[:], in_=bank[:], func=ACT.Square, accum_out=acc)
 
-        def inv_rms(ss, name):
-            inv = const.tile(list(ss.shape), F32, name=name + "_inv")
-            nc.scalar.activation(out=inv[:], in_=ss, func=ACT.Abs_reciprocal_sqrt, scale=1.0 / DH, bias=EPS)
-            return inv
+        def inv_rms(out, ss):
+            nc.scalar.activation(out=out, in_=ss, func=ACT.Abs_reciprocal_sqrt, scale=1.0 / DH, bias=EPS)
 
-        def norms(a):
-            ss = work.tile([P, H], F32, name="ss", tag="ss", bufs=NT + 2)
-            inv = work.tile([P, H], F32, name="inv", tag="inv", bufs=NT + 2)
-            lc, ls = x_cols(a)
-            for g in range(H):
-                bank = bank_tile([P, 512], "sq")
-                mx(bank[:], lc, ls, wc[g][:], ws[g][:])
-                sum_squares(bank, ss[:, g : g + 1])
-                if a == 0:
-                    nc.scalar.activation(
-                        out=inv[:, g : g + 1], in_=ss[:, g : g + 1], func=ACT.Abs_reciprocal_sqrt, scale=1.0 / DH, bias=EPS
-                    )
-            if a > 0:
-                nc.scalar.activation(out=inv[:], in_=ss[:], func=ACT.Abs_reciprocal_sqrt, scale=1.0 / DH, bias=EPS)
-            return inv
+        kg = const.tile([P, 2, 3], F32, name="kg")
 
-        def k_norms(th):
-            ss = work.tile([P, H], F32, name="ss", tag="ss", bufs=NT + 2)
-            inv = work.tile([P, H], F32, name="inv", tag="inv", bufs=NT + 2)
-            for tb in range(4):
-                lc, ls = x_cols(4 * th + tb)
-                bank = bank_tile([P, 512], "sq")
-                mx(bank[:], lc, ls, wc[H][:], ws[H][:])
-                sum_squares(bank, ss[:, tb : tb + 1])
-            nc.scalar.activation(out=inv[:], in_=ss[:], func=ACT.Abs_reciprocal_sqrt, scale=1.0 / DH, bias=EPS)
-            return inv
+        def k_bank(th, j, e):
+            u = v_tile([P, 512], "ukt")
+            csl = slice(256 * j + P * e, 256 * j + P * (e + 1))
+            mx(u[:], wc[4][:, csl], ws[4][:, csl], xc[:, half[th]], xs[:, half[th]])
+            return u
 
-        def k_products(th):
-            pr = []
-            for q in range(4):
-                pr.append(work.tile([P, 2, 512], F32, name="pr%d" % q, tag="pr%d" % q, bufs=1))
-            tsl = slice(512 * th, 512 * (th + 1))
-            for j in range(2):
-                ue = []
-                for e in range(2):
-                    u = bank_tile([P, 512], "ukt")
-                    csl = slice(256 * j + P * e, 256 * j + P * (e + 1))
-                    mx(u[:], wc[4][:, csl], ws[4][:, csl], xc[:, tsl], xs[:, tsl])
-                    ue.append(u)
-                for q, (e, gi, tab) in enumerate(((0, 0, cosT), (1, 2, sinT), (0, 1, sinT), (1, 1, cosT))):
-                    nc.vector.scalar_tensor_tensor(
-                        out=pr[q][:, j, :], in0=ue[e][:], scalar=kg[:, j, gi : gi + 1], in1=tab[:, j, tsl],
-                        op0=ALU.mult, op1=ALU.mult,
-                    )
-            zs = []
-            for e in range(2):
-                z = work.tile([P, 2, 512], F32, name="zk%d" % e, tag="zk%d" % e, bufs=2)
-                nc.gpsimd.tensor_tensor(out=z[:], in0=pr[2 * e][:], in1=pr[2 * e + 1][:], op=ALU.add)
-                zs.append(z)
-            return zs
+        def k_product_tiles():
+            return [work.tile([P, 2, 512], F32, name="pr%d" % q, tag="pr%d" % q, bufs=PRB) for q in range(4)]
 
-        def k_finish(th, pr, inv):
-            for tb in range(4):
-                a = 4 * th + tb
-                yb = bank_tile([P, 512], "ykb")
-                for j in range(2):
-                    for e in range(2):
-                        o = yb[:, 256 * j + P * e : 256 * j + P * (e + 1)]
-                        nc.tensor.transpose(o, pr[e][:, j, P * tb : P * (tb + 1)], ident[:])
-                yk = work.tile([P, DH], F32, name="yk", tag="yk", bufs=4)
-                nc.scalar.activation(
-                    out=yk[:].rearrange("p (j i e) -> p j i e", j=2, e=2),
-                    in_=yb[:].rearrange("p (j e i) -> p j i e", j=2, e=2),
-                    func=ACT.Copy, scale=inv[:, tb : tb + 1],
+        def k_products(th, j, e, u, pr):
+            for q, gi, tab in (((0, 0, cosT), (2, 1, sinT)), ((1, 2, sinT), (3, 1, cosT)))[e]:
+                nc.vector.scalar_tensor_tensor(
+                    out=pr[q][:, j, :], in0=u[:], scalar=kg[:, j, gi : gi + 1], in1=tab[th][:, j, :],
+                    op0=ALU.mult, op1=ALU.mult,
                 )
-                nc.sync.dma_start(out=o1[:, a, :], in_=yk[:])
 
-        def values(a):
-            bank = bank_tile([P, 512], "vb")
+        def k_turn(a, pr):
+            yb = s_tile([P, 512], "ykb")
+            tb = a % 4
+            for j in range(2):
+                for e in range(2):
+                    for m in range(2):
+                        nc.tensor.matmul(
+                            out=yb[:, 256 * j + P * e : 256 * j + P * (e + 1)], lhsT=pr[2 * e + m][:, j, P * tb : P * (tb + 1)],
+                            rhs=ident[:], is_transpose=True, start=(m == 0), stop=(m == 1),
+                        )
+            return yb
+
+        def k_out(a, yb):
+            yk = work.tile([P, DH], F32, name="yk", tag="yk", bufs=4)
+            nc.scalar.activation(
+                out=yk[:].rearrange("p (j i e) -> p j i e", j=2, e=2), in_=yb[:].rearrange("p (j e i) -> p j i e", j=2, e=2),
+                func=ACT.Copy, scale=invk[:, a : a + 1],
+            )
+            nc.sync.dma_start(out=o1[:, a, :], in_=yk[:])
+
+        def v_bank(a):
+            bank = s_tile([P, 512], "vbk")
             lc, ls = x_cols(a)
             mx(bank[:], lc, ls, wc[5][:], ws[5][:])
+            return bank
+
+        def v_out(a, bank):
             vs = work.tile([P, DH], F32, name="vs", tag="vs", bufs=4)
-            if VALV:
-                nc.vector.tensor_copy(out=vs[:], in_=bank[:])
-            else:
-                nc.scalar.copy(out=vs[:], in_=bank[:])
+            nc.scalar.copy(out=vs[:], in_=bank[:])
             nc.sync.dma_start(out=o2[:, a, :], in_=vs[:])
 
-        def q_tables(a):
-            ps = bank_tile([P, 2, 2, P], "tab_ps")
-            for r, src in enumerate((cosT, sinT)):
+        def table_bank(a):
+            ps = v_tile([P, 2, 2, P], "tab_ps")
+            th, c = divmod(a, 4)
+            for r, src in enumerate((cosT[th], sinT[th])):
                 for j in range(2):
-                    nc.tensor.transpose(ps[:, r, j, :], src[:, j, P * a : P * (a + 1)], ident[:])
-            tab = work.tile([P, 2, DH], F32, name="tab", tag="tab", bufs=3)
+                    nc.tensor.transpose(ps[:, r, j, :], src[:, j, P * c : P * (c + 1)], ident[:])
+            return ps
+
+        qg = const.tile([P, 2, 3], F32, name="qg")
+
+        def gain_tables(th):
+            out = [[], []]
+            for r, src in enumerate((cosT[th], sinT[th])):
+                for e in range(2):
+                    gt = const.tile([P, 2, HT], F32, name="gt%d%d%d" % (th, r, e))
+                    gi = e if r == 0 else (1, 2)[e]
+                    for j in range(2):
+                        nc.gpsimd.tensor_scalar(out=gt[:, j, :], in0=src[:, j, :], scalar1=qg[:, j, gi : gi + 1], scalar2=0.0, op0=ALU.mult, op1=ALU.add)
+                    out[r].append(gt)
+            return out
+
+        def gain_bank(a, r, gt):
+            ps = s_tile([P, 2, 2, P], "gtab_ps")
+            c = a % 4
+            for e in range(2):
+                for j in range(2):
+                    nc.tensor.transpose(ps[:, e, j, :], gt[r][e][:, j, P * c : P * (c + 1)], ident[:])
+            return ps
+
+        def gain_out(ps, tab, r):
+            nc.scalar.copy(
+                out=tab[:, r, :].rearrange("p (j i e) -> p j i e", j=2, e=2), in_=ps[:].rearrange("p e j i -> p j i e")
+            )
+
+        def table(ps):
+            tab = work.tile([P, 2, DH], F32, name="tab", tag="tab", bufs=TABB)
             nc.vector.tensor_tensor(
                 out=tab[:].rearrange("p r (i e) -> p (r i) e", e=2),
                 in0=ps[:].rearrange("p r j i -> p (r j i)").unsqueeze(2).to_broadcast([P, DH, 2]),
@@ -310,52 +322,230 @@ def tile_attention_pa_kernel(tc, x, wq_bytes, wq_scale, wkv, q_norm_w, k_norm_w,
             )
             return tab
 
-        def queries(a, tab, inv):
+        def q_bank(n):
+            a, h = divmod(n, H)
+            bank = v_tile([P, 512], "qb")
             lc, ls = x_cols(a)
-            for h in range(H):
-                bank = bank_tile([P, 512], "qb")
-                mx(bank[:], lc, ls, wc[h][:], ws[h][:])
-                t12 = work.tile([P, 2, DH], F32, name="t12", tag="t12", bufs=4)
-                y = work.tile([P, DH], F32, name="y", tag="y", bufs=8)
-                nc.vector.scalar_tensor_tensor(
-                    out=t12[:], in0=bank[:].unsqueeze(1).to_broadcast([P, 2, DH]), scalar=inv[:, h : h + 1],
-                    in1=tab[:], op0=ALU.mult, op1=ALU.mult,
-                )
-                nc.gpsimd.tensor_tensor(
-                    out=y[:].rearrange("p (i e) -> p i e", e=2),
-                    in0=t12[:, 0, :].rearrange("p (i e) -> p i e", e=2),
-                    in1=t12[:, 1, :].rearrange("p (i e) -> p i e", e=2)[:, :, ::-1],
-                    op=ALU.add,
-                )
-                nc.sync.dma_start(out=o0[:, h * NT + a, :], in_=y[:])
+            mx(bank[:], lc, ls, wc[h][:], ws[h][:])
+            return bank
 
-        x_prep(0)
-        for h in range(H):
-            wq_prep(h)
-        invs = [norms(0)]
-        tabs = [q_tables(0)]
-        wk_prep()
-        x_prep(1)
-        for a in range(NT):
-            if a + 1 < NT:
-                invs.append(norms(a + 1))
-                tabs.append(q_tables(a + 1))
-            queries(a, tabs[a], invs[a])
-            if a == 0:
-                pr0 = k_products(0)
-            elif a == 1:
-                pr1 = k_products(1)
-                invk0 = k_norms(0)
-            elif a == 2:
-                wv_prep()
-                for v in range(4):
-                    values(v)
-            elif a == 3:
-                k_finish(0, pr0, invk0)
-            elif a == 4:
-                invk1 = k_norms(1)
-            elif a == 5:
-                for v in range(4, NT):
-                    values(v)
-            elif a == 6:
-                k_finish(1, pr1, invk1)
+        def query_pair(n, tab):
+            return work.tile([P, 2, 2, DH], F32, name="t12", tag="t12", bufs=T12B)
+
+        def query(n, bank, tab, t12):
+            a, h = divmod(n, H)
+            nc.vector.scalar_tensor_tensor(
+                out=t12[:, h % 2], in0=bank[:].unsqueeze(1).to_broadcast([P, 2, DH]), scalar=inv[a][:, h : h + 1],
+                in1=tab[:], op0=ALU.mult, op1=ALU.mult,
+            )
+
+        def query_out(n, t12, count, on_vector):
+            a, h = divmod(n, H)
+            s = h % 2
+            y = work.tile([P, 2, DH], F32, name="y", tag="y", bufs=YB)
+            (nc.vector if on_vector else nc.gpsimd).tensor_tensor(
+                out=y[:, s : s + count].rearrange("p h (i e) -> p h i e", e=2),
+                in0=t12[:, s : s + count, 0, :].rearrange("p h (i e) -> p h i e", e=2),
+                in1=t12[:, s : s + count, 1, :].rearrange("p h (i e) -> p h i e", e=2)[:, :, :, ::-1],
+                op=ALU.add,
+            )
+            nc.sync.dma_start(out=o0v[:, h : h + count, a, :], in_=y[:, s : s + count])
+
+        def wq_widen(h):
+            return [widen(h, b) for b in range(2)]
+
+        def wq_turn(wide, on_vector=False):
+            grp, grpw = group_tile()
+            for b in range(2):
+                exit_plain(turn_pair(wide[b][0][:], wide[b][1][:], on_vector), grpw, b, on_vector)
+            return grp
+
+        def wq_quant(h, grp):
+            quantise(grp, wc[h][:], ws[h][:])
+
+        def norm_sq(a, h):
+            square(square_bank(a, h), ssq[a][:, h : h + 1])
+
+        def norm(a, h):
+            square(square_bank(a, h), ssq[a][:, h : h + 1])
+            inv_rms(inv[a][:, h : h + 1], ssq[a][:, h : h + 1])
+
+        tabs = {}
+        pair = {}
+
+        def do_query(n, bank):
+            a, h = divmod(n, H)
+            if n not in pair:
+                pair[n] = query_pair(n, None)
+                pair[n + 1] = pair[n]
+            query(n, bank, tabs[a], pair[n])
+            if n in SOLO:
+                query_out(n, pair[n], 1, n in VADD)
+            elif h % 2 == 1:
+                query_out(n - 1, pair[n], 2, n in VADD)
+
+        turns0 = turns_of(0)
+        xg0 = x_turn(0, False)
+        frac0 = fractions(0, turns0)
+        scale_ps = v_tile([P, D], "scale_ps")
+        nc.tensor.matmul(out=scale_ps[:], lhsT=ones_sq[:], rhs=scale_row[:], start=True, stop=True)
+        x_quant(0, xg0)
+        nc.vector.tensor_copy(out=scale_sb[:], in_=scale_ps[:])
+        sin_cos(0, frac0)
+        turns1 = turns_of(1)
+        g0 = wq_turn(wq_widen(0))
+        frac1 = fractions(1, turns1)
+        kgrp, kgrpw = group_tile()
+        for j, bank in enumerate(wkv_turn(0)):
+            exit_split(bank, kgrpw, j)
+        g1 = wq_turn(wq_widen(1))
+        nc.vector.tensor_copy(out=kg[:, :, 0:2], in_=kgain_bf[:])
+        nc.vector.tensor_scalar(out=kg[:, :, 2], in0=kgain_bf[:, :, 0], scalar1=-1.0, scalar2=None, op0=ALU.mult)
+        quantise(kgrp, wc[4][:], ws[4][:])
+        kb = [k_bank(0, 0, e) for e in range(2)]
+        wq_quant(0, g0)
+        sin_cos(1, frac1)
+        nc.scalar.activation(out=warm[:, 1:2], in_=cosT[1][:, 1, HT - 1 : HT], func=ACT.Abs_reciprocal_sqrt, scale=0.0, bias=1.0)
+        pr0 = k_product_tiles()
+        tb0 = table_bank(0)
+        norm(0, 0)
+        q0 = q_bank(0)
+        for i in range(2):
+            k_products(0, 0, i, kb[i], pr0)
+        w2 = wq_widen(2)
+        norm(1, 0)
+        gpv = gq[:, 0, :].rearrange("p (i e) -> p i e", e=2)
+        gqv = gq[:, 1, :].rearrange("p (i e) -> p i e", e=2)
+        nc.vector.tensor_copy(out=gqv[:, :, 0], in_=gpv[:, :, 1])
+        nc.vector.tensor_scalar(out=gqv[:, :, 1], in0=gpv[:, :, 0], scalar1=-1.0, scalar2=None, op0=ALU.mult)
+        nc.vector.tensor_copy(out=qg[:, :, 0:2], in_=qgain_bf[:])
+        nc.vector.tensor_scalar(out=qg[:, :, 2], in0=qgain_bf[:, :, 0], scalar1=-1.0, scalar2=None, op0=ALU.mult)
+        wq_quant(1, g1)
+        tabs[0] = table(tb0)
+        g2 = wq_turn(w2)
+        norm(0, 1)
+        do_query(0, q0)
+        q1 = q_bank(1)
+        norm(1, 1)
+        for a in range(4):
+            square(square_bank(a, H), ssk[:, a : a + 1])
+        inv_rms(invk[:, 0:4], ssk[:, 0:4])
+        w3 = wq_widen(3)
+        tb1 = table_bank(1)
+        kb = [k_bank(0, 1, e) for e in range(2)]
+        do_query(1, q1)
+        wq_quant(2, g2)
+        g3 = wq_turn(w3)
+        norm(0, 2)
+        q2 = q_bank(2)
+        k_products(0, 1, 0, kb[0], pr0)
+        norm(1, 2)
+        do_query(2, q2)
+        wq_quant(3, g3)
+        norm(0, 3)
+        norm(1, 3)
+        q3 = q_bank(3)
+        k_products(0, 1, 1, kb[1], pr0)
+        tabs[1] = table(tb1)
+        q4 = q_bank(4)
+        xg1 = x_turn(1, False)
+        do_query(3, q3)
+        vg, vgw = group_tile()
+        for b, bank in enumerate(wkv_turn(1)):
+            exit_plain(bank, vgw, b, False)
+        q5 = q_bank(5)
+        for h in range(4):
+            norm_sq(2, h)
+        inv_rms(inv[2][:], ssq[2][:])
+        do_query(4, q4)
+        tb2 = table_bank(2)
+        q6 = q_bank(6)
+        x_quant(1, xg1)
+        do_query(5, q5)
+        q7 = q_bank(7)
+        for h in range(4):
+            norm_sq(3, h)
+        inv_rms(inv[3][:], ssq[3][:])
+        tabs[2] = table(tb2)
+        quantise(vg, wc[5][:], ws[5][:])
+        do_query(6, q6)
+        vq = []
+        sq = []
+
+        def push(stream, look, fill, drain):
+            stream.append((fill(), drain))
+            settle(stream, look)
+
+        def settle(stream, look):
+            while len(stream) > look:
+                bank, drain = stream[0]
+                stream.remove(stream[0])
+                drain(bank)
+
+        def push_query(n):
+            push(vq, VR - 1, lambda: q_bank(n), lambda bank: do_query(n, bank))
+
+        def push_table(a):
+            def drain(bank):
+                tabs[a] = table(bank)
+            push(vq, VR - 1, lambda: table_bank(a), drain)
+
+        def push_gain(a, r):
+            if r == 0:
+                tabs[a] = work.tile([P, 2, DH], F32, name="tab", tag="tab", bufs=TABB)
+            push(sq, SR - 1, lambda: gain_bank(a, r, gts[a // 4]), lambda bank: gain_out(bank, tabs[a], r))
+
+        def push_k(th, j, e, pr):
+            push(vq, VR - 1, lambda: k_bank(th, j, e), lambda bank: k_products(th, j, e, bank, pr))
+
+        def push_norm(a, h):
+            def drain(bank):
+                square(bank, ssq[a][:, h : h + 1])
+                if h == H - 1:
+                    inv_rms(inv[a][:], ssq[a][:])
+            push(sq, SR - 1, lambda: square_bank(a, h), drain)
+
+        def push_k_norm(a):
+            def drain(bank):
+                square(bank, ssk[:, a : a + 1])
+                if a % 4 == 3:
+                    inv_rms(invk[:, a - 3 : a + 1], ssk[:, a - 3 : a + 1])
+            push(sq, SR - 1, lambda: square_bank(a, H), drain)
+
+        def push_k_out(a):
+            push(sq, SR - 1, lambda: k_turn(a, prs[a // 4]), lambda bank: k_out(a, bank))
+
+        def push_v_out(a):
+            push(sq, SR - 1, lambda: v_bank(a), lambda bank: v_out(a, bank))
+
+
+        prs = [pr0, None]
+        gts = [None, None]
+        todo = [lambda a=a: push_k_out(a) for a in range(4)]
+
+        def norms_and_table(a):
+            return [lambda h=h: push_norm(a, h) for h in range(H)] + [lambda r=r: push_gain(a, r) for r in range(2)]
+        todo += norms_and_table(4) + norms_and_table(5) + norms_and_table(6)
+        todo += [lambda a=a: push_k_norm(a) for a in range(4, 8)]
+        todo += norms_and_table(7)
+        todo += [lambda a=a: push_k_out(a) for a in range(4, 8)]
+        todo += [lambda a=a: push_v_out(a) for a in range(8)]
+        vq.append((q7, lambda bank: do_query(7, bank)))
+        count = 0
+        for n in range(8, NQ):
+            for f in todo[0:2]:
+                f()
+            todo = todo[2:]
+            a, h = divmod(n, H)
+            push_query(n)
+            if n == 9:
+                push_table(3)
+            if n == 8:
+                prs[1] = k_product_tiles()
+                for i in range(4):
+                    push_k(1, i // 2, i % 2, prs[1])
+                gts[1] = gain_tables(1)
+        for f in todo:
+            f()
+        settle(sq, 0)
+        settle(vq, 0)

@@ -28,13 +28,12 @@ TWO_PI = 2.0 * math.pi
 
 VR = 4
 SR = 4
-VADD = (NQ - 1,)
+VADD = ()
 SOLO = (NQ - 2, NQ - 1)
 PRB = 2
-TABB = 4
 T12B = 3
-YB = 4
-GT0 = 4
+YB = 5
+TABB = 4
 
 FLOPS = 2 * T * D * (H * DH + 2 * DH)
 
@@ -61,54 +60,59 @@ def tile_attention_pa_kernel(tc, x, wq_bytes, wq_scale, wkv, q_norm_w, k_norm_w,
         wkv_sb = []
         wq_b8 = []
         for c in range(2):
-            x_sb.append(const.tile([P, 4, D], BF16, name="x_sb%d" % c))
-            wkv_sb.append(const.tile([P, 4, D], BF16, name="wkv_sb%d" % c))
+            x_sb.append(const.tile([P, 4, D], BF16, name="x_sb%d" % c, tag="early%d" % c))
+            wkv_sb.append(const.tile([P, 4, D], BF16, name="wkv_sb%d" % c, tag="early%d" % (2 + c)))
         for c in range(H):
             wq_b8.append(const.tile([P, 4, D], U8, name="wq_b8_%d" % c))
         scale_row = const.tile([P, D], F32, name="scale_row")
         ident = const.tile([P, P], F32, name="ident")
         trow = [const.tile([P, HT], F32, name="trow%d" % th) for th in range(2)]
         make_identity(nc, ident[:])
-        nc.gpsimd.memset(scale_row[:], 0.0)
         nc.gpsimd.iota(trow[0][:], pattern=[[1, HT]], base=0, channel_multiplier=0, allow_small_or_imprecise_dtypes=True)
         gq = const.tile([P, 2, DH], BF16, name="gq")
-        kgain_bf = const.tile([P, 2, 2], BF16, name="kgain_bf")
-        qgain_bf = const.tile([P, 2, 2], BF16, name="qgain_bf")
+        one = const.tile([P, 1], F32, name="one")
+        nc.vector.memset(one[:], 1.0)
+        nc.vector.memset(scale_row[:], 0.0)
+        gain_row = const.tile([P, 2, DH], BF16, name="gain_row")
+        sign = const.tile([P, 2], BF16, name="sign")
+        nc.vector.memset(gain_row[:], 0.0)
+        nc.vector.memset(sign[:, 0:1], 1.0)
+        nc.vector.memset(sign[:, 1:2], -1.0)
+        gains = const.tile([P, 2, 2, 3], F32, name="gains")
+        qg = gains[:, 0]
+        kg = gains[:, 1]
         nc.sync.dma_start(out=x_sb[0][:], in_=xv[:, 0:4, :])
         nc.sync.dma_start(out=scale_row[0:1, :], in_=wq_scale)
         nc.sync.dma_start(out=wq_b8[0][:], in_=wqv[:, 0:4, :])
         nc.sync.dma_start(out=wkv_sb[0][:], in_=wkvv[:, 0:4, :])
+        nc.sync.dma_start(out=gain_row[0:1, 0, :], in_=q_norm_w.rearrange("(o d) -> o d", o=1))
+        nc.sync.dma_start(out=gain_row[0:1, 1, :], in_=k_norm_w.rearrange("(o d) -> o d", o=1))
         nc.sync.dma_start(out=wq_b8[1][:], in_=wqv[:, 4:8, :])
-        nc.sync.dma_start(out=kgain_bf[:], in_=k_norm_w.rearrange("(j p e) -> p j e", j=2, e=2))
-        nc.sync.dma_start(out=qgain_bf[:], in_=q_norm_w.rearrange("(j p e) -> p j e", j=2, e=2))
-        nc.sync.dma_start(out=gq[:, 0, :], in_=q_norm_w.partition_broadcast(P))
         nc.sync.dma_start(out=wq_b8[2][:], in_=wqv[:, 8:12, :])
         nc.sync.dma_start(out=wq_b8[3][:], in_=wqv[:, 12:16, :])
         nc.sync.dma_start(out=x_sb[1][:], in_=xv[:, 4:8, :])
         nc.sync.dma_start(out=wkv_sb[1][:], in_=wkvv[:, 4:8, :])
+        nc.sync.dma_start(out=gq[:, 0, :], in_=q_norm_w.partition_broadcast(P))
 
         o0v = out_0.rearrange("b h (a p) d -> p (b h) a d", p=P)
         o1 = out_1.rearrange("b (a p) d -> p (b a) d", p=P)
         o2 = out_2.rearrange("b (a p) d -> p (b a) d", p=P)
 
-        one = const.tile([P, 1], F32, name="one")
-        nc.vector.memset(one[:], 1.0)
         warm = const.tile([P, 2], F32, name="warm")
-        nc.scalar.activation(out=warm[:, 0:1], in_=one[:], func=ACT.Sin)
         grow = const.tile([P, 256], F32, name="grow")
-        nc.vector.tensor_scalar(out=grow[:, 0:1], in0=one[:], scalar1=1.0 / TWO_PI, scalar2=None, op0=ALU.mult)
+        nc.scalar.activation(out=grow[:, 0:1], in_=one[:], func=ACT.Copy, scale=1.0 / TWO_PI)
         for level in range(4):
             w = 4 ** level
             for m in range(1, 4):
-                nc.vector.tensor_scalar(
-                    out=grow[:, m * w : (m + 1) * w], in0=grow[:, 0:w], scalar1=ROPE_BASE ** (-m * w / 256.0), scalar2=None,
-                    op0=ALU.mult,
+                nc.scalar.activation(
+                    out=grow[:, m * w : (m + 1) * w], in_=grow[:, 0:w], func=ACT.Copy, scale=ROPE_BASE ** (-m * w / 256.0)
                 )
-        gps = s_tile([P, 2, P], "gps")
+        nc.scalar.activation(out=warm[:, 0:1], in_=one[:], func=ACT.Sin)
+        gps = v_tile([P, 2, P], "gps")
         for j in range(2):
             nc.tensor.transpose(gps[:, j, :], grow[:, P * j : P * (j + 1)], ident[:])
         gcol = const.tile([P, 2], F32, name="gcol")
-        nc.scalar.copy(out=gcol[:], in_=gps[:, :, 0])
+        nc.vector.tensor_copy(out=gcol[:], in_=gps[:, :, 0])
         ones_sq = const.tile([P, P], F32, name="ones_sq")
         nc.vector.memset(ones_sq[:], 1.0)
         scale_sb = const.tile([P, D], F32, name="scale_sb")
@@ -116,13 +120,23 @@ def tile_attention_pa_kernel(tc, x, wq_bytes, wq_scale, wkv, q_norm_w, k_norm_w,
         sinT = [const.tile([P, 2, HT], F32, name="sinT%d" % th) for th in range(2)]
         cosT = [const.tile([P, 2, HT], F32, name="cosT%d" % th) for th in range(2)]
         half = [slice(0, HT), slice(HT, T)]
-        nc.vector.tensor_scalar(out=trow[1][:], in0=trow[0][:], scalar1=float(HT), scalar2=None, op0=ALU.add)
+
+        def load_gains():
+            ps = s_tile([P, 2, 2, 3], "gain_ps")
+            for r in range(2):
+                for j in range(2):
+                    for c, (e, s) in enumerate(((0, 0), (1, 0), (0, 1))):
+                        nc.tensor.matmul(
+                            out=ps[:, r, j, c : c + 1], lhsT=gain_row[:, r, 256 * j + e : 256 * (j + 1) : 2], rhs=sign[:, s : s + 1],
+                            start=True, stop=True,
+                        )
+            nc.scalar.copy(out=gains[:], in_=ps[:])
 
         def turns_of(th):
             tiles = []
             for j in range(2):
                 turns = stage.tile([P, HT], I32, name="turns", tag="turns", bufs=4)
-                nc.gpsimd.tensor_scalar(
+                nc.vector.tensor_scalar(
                     out=turns[:], in0=trow[th][:], scalar1=gcol[:, j : j + 1], scalar2=0.0, op0=ALU.mult, op1=ALU.add
                 )
                 tiles.append(turns)
@@ -229,8 +243,6 @@ def tile_attention_pa_kernel(tc, x, wq_bytes, wq_scale, wkv, q_norm_w, k_norm_w,
         def inv_rms(out, ss):
             nc.scalar.activation(out=out, in_=ss, func=ACT.Abs_reciprocal_sqrt, scale=1.0 / DH, bias=EPS)
 
-        kg = const.tile([P, 2, 3], F32, name="kg")
-
         def k_bank(th, j, e):
             u = v_tile([P, 512], "ukt")
             csl = slice(256 * j + P * e, 256 * j + P * (e + 1))
@@ -286,16 +298,14 @@ def tile_attention_pa_kernel(tc, x, wq_bytes, wq_scale, wkv, q_norm_w, k_norm_w,
                     nc.tensor.transpose(ps[:, r, j, :], src[:, j, P * c : P * (c + 1)], ident[:])
             return ps
 
-        qg = const.tile([P, 2, 3], F32, name="qg")
-
         def gain_tables(th):
             out = [[], []]
             for r, src in enumerate((cosT[th], sinT[th])):
                 for e in range(2):
-                    gt = const.tile([P, 2, HT], F32, name="gt%d%d%d" % (th, r, e))
+                    gt = const.tile([P, 2, HT], F32, name="gt%d%d%d" % (th, r, e), tag="early%d" % (2 * r + e))
                     gi = e if r == 0 else (1, 2)[e]
                     for j in range(2):
-                        nc.gpsimd.tensor_scalar(out=gt[:, j, :], in0=src[:, j, :], scalar1=qg[:, j, gi : gi + 1], scalar2=0.0, op0=ALU.mult, op1=ALU.add)
+                        nc.scalar.activation(out=gt[:, j, :], in_=src[:, j, :], func=ACT.Copy, scale=qg[:, j, gi : gi + 1])
                     out[r].append(gt)
             return out
 
@@ -389,18 +399,18 @@ def tile_attention_pa_kernel(tc, x, wq_bytes, wq_scale, wkv, q_norm_w, k_norm_w,
         frac0 = fractions(0, turns0)
         scale_ps = v_tile([P, D], "scale_ps")
         nc.tensor.matmul(out=scale_ps[:], lhsT=ones_sq[:], rhs=scale_row[:], start=True, stop=True)
+        nc.vector.tensor_scalar(out=trow[1][:], in0=trow[0][:], scalar1=float(HT), scalar2=None, op0=ALU.add)
+        turns1 = turns_of(1)
         x_quant(0, xg0)
         nc.vector.tensor_copy(out=scale_sb[:], in_=scale_ps[:])
         sin_cos(0, frac0)
-        turns1 = turns_of(1)
         g0 = wq_turn(wq_widen(0))
         frac1 = fractions(1, turns1)
         kgrp, kgrpw = group_tile()
         for j, bank in enumerate(wkv_turn(0)):
             exit_split(bank, kgrpw, j)
+        load_gains()
         g1 = wq_turn(wq_widen(1))
-        nc.vector.tensor_copy(out=kg[:, :, 0:2], in_=kgain_bf[:])
-        nc.vector.tensor_scalar(out=kg[:, :, 2], in0=kgain_bf[:, :, 0], scalar1=-1.0, scalar2=None, op0=ALU.mult)
         quantise(kgrp, wc[4][:], ws[4][:])
         kb = [k_bank(0, 0, e) for e in range(2)]
         wq_quant(0, g0)
@@ -408,67 +418,62 @@ def tile_attention_pa_kernel(tc, x, wq_bytes, wq_scale, wkv, q_norm_w, k_norm_w,
         nc.scalar.activation(out=warm[:, 1:2], in_=cosT[1][:, 1, HT - 1 : HT], func=ACT.Abs_reciprocal_sqrt, scale=0.0, bias=1.0)
         pr0 = k_product_tiles()
         tb0 = table_bank(0)
-        norm(0, 0)
-        q0 = q_bank(0)
         for i in range(2):
             k_products(0, 0, i, kb[i], pr0)
-        w2 = wq_widen(2)
-        norm(1, 0)
+        g2 = wq_turn(wq_widen(2))
+        norm(0, 0)
+        kb = [k_bank(0, 1, e) for e in range(2)]
+        wq_quant(1, g1)
+        q0 = q_bank(0)
+        g3 = wq_turn(wq_widen(3))
+        norm(0, 1)
         gpv = gq[:, 0, :].rearrange("p (i e) -> p i e", e=2)
         gqv = gq[:, 1, :].rearrange("p (i e) -> p i e", e=2)
         nc.vector.tensor_copy(out=gqv[:, :, 0], in_=gpv[:, :, 1])
         nc.vector.tensor_scalar(out=gqv[:, :, 1], in0=gpv[:, :, 0], scalar1=-1.0, scalar2=None, op0=ALU.mult)
-        nc.vector.tensor_copy(out=qg[:, :, 0:2], in_=qgain_bf[:])
-        nc.vector.tensor_scalar(out=qg[:, :, 2], in0=qgain_bf[:, :, 0], scalar1=-1.0, scalar2=None, op0=ALU.mult)
-        wq_quant(1, g1)
         tabs[0] = table(tb0)
-        g2 = wq_turn(w2)
-        norm(0, 1)
-        do_query(0, q0)
-        q1 = q_bank(1)
-        norm(1, 1)
-        for a in range(4):
-            square(square_bank(a, H), ssk[:, a : a + 1])
-        inv_rms(invk[:, 0:4], ssk[:, 0:4])
-        w3 = wq_widen(3)
-        tb1 = table_bank(1)
-        kb = [k_bank(0, 1, e) for e in range(2)]
-        do_query(1, q1)
         wq_quant(2, g2)
-        g3 = wq_turn(w3)
+        q1 = q_bank(1)
         norm(0, 2)
-        q2 = q_bank(2)
-        k_products(0, 1, 0, kb[0], pr0)
-        norm(1, 2)
-        do_query(2, q2)
-        wq_quant(3, g3)
-        norm(0, 3)
-        norm(1, 3)
-        q3 = q_bank(3)
-        k_products(0, 1, 1, kb[1], pr0)
-        tabs[1] = table(tb1)
-        q4 = q_bank(4)
         xg1 = x_turn(1, False)
-        do_query(3, q3)
+        k_products(0, 1, 0, kb[0], pr0)
+        wq_quant(3, g3)
+        q2 = q_bank(2)
+        norm(0, 3)
+        k_products(0, 1, 1, kb[1], pr0)
+        x_quant(1, xg1)
+        q3 = q_bank(3)
         vg, vgw = group_tile()
         for b, bank in enumerate(wkv_turn(1)):
             exit_plain(bank, vgw, b, False)
+        do_query(0, q0)
+        tb1 = table_bank(1)
+        for h in range(4):
+            norm_sq(1, h)
+        inv_rms(inv[1][:], ssq[1][:])
+        do_query(1, q1)
+        q4 = q_bank(4)
+        do_query(2, q2)
         q5 = q_bank(5)
         for h in range(4):
             norm_sq(2, h)
         inv_rms(inv[2][:], ssq[2][:])
-        do_query(4, q4)
-        tb2 = table_bank(2)
+        do_query(3, q3)
         q6 = q_bank(6)
-        x_quant(1, xg1)
-        do_query(5, q5)
+        tabs[1] = table(tb1)
+        tb2 = table_bank(2)
+        do_query(4, q4)
         q7 = q_bank(7)
         for h in range(4):
             norm_sq(3, h)
         inv_rms(inv[3][:], ssq[3][:])
+        do_query(5, q5)
         tabs[2] = table(tb2)
         quantise(vg, wc[5][:], ws[5][:])
         do_query(6, q6)
+        for a in range(4):
+            square(square_bank(a, H), ssk[:, a : a + 1])
+        inv_rms(invk[:, 0:4], ssk[:, 0:4])
         vq = []
         sq = []
 
@@ -483,69 +488,77 @@ def tile_attention_pa_kernel(tc, x, wq_bytes, wq_scale, wkv, q_norm_w, k_norm_w,
                 drain(bank)
 
         def push_query(n):
-            push(vq, VR - 1, lambda: q_bank(n), lambda bank: do_query(n, bank))
+            push(vq, 3, lambda: q_bank(n), lambda bank: do_query(n, bank))
 
         def push_table(a):
             def drain(bank):
                 tabs[a] = table(bank)
-            push(vq, VR - 1, lambda: table_bank(a), drain)
+            push(vq, 3, lambda: table_bank(a), drain)
 
         def push_gain(a, r):
             if r == 0:
                 tabs[a] = work.tile([P, 2, DH], F32, name="tab", tag="tab", bufs=TABB)
-            push(sq, SR - 1, lambda: gain_bank(a, r, gts[a // 4]), lambda bank: gain_out(bank, tabs[a], r))
+            push(sq, 2, lambda: gain_bank(a, r, gts[a // 4]), lambda bank: gain_out(bank, tabs[a], r))
 
         def push_k(th, j, e, pr):
-            push(vq, VR - 1, lambda: k_bank(th, j, e), lambda bank: k_products(th, j, e, bank, pr))
+            push(vq, 3, lambda: k_bank(th, j, e), lambda bank: k_products(th, j, e, bank, pr))
 
         def push_norm(a, h):
             def drain(bank):
                 square(bank, ssq[a][:, h : h + 1])
                 if h == H - 1:
                     inv_rms(inv[a][:], ssq[a][:])
-            push(sq, SR - 1, lambda: square_bank(a, h), drain)
+            push(sq, 2, lambda: square_bank(a, h), drain)
 
         def push_k_norm(a):
             def drain(bank):
                 square(bank, ssk[:, a : a + 1])
                 if a % 4 == 3:
                     inv_rms(invk[:, a - 3 : a + 1], ssk[:, a - 3 : a + 1])
-            push(sq, SR - 1, lambda: square_bank(a, H), drain)
+            push(sq, 2, lambda: square_bank(a, H), drain)
 
         def push_k_out(a):
-            push(sq, SR - 1, lambda: k_turn(a, prs[a // 4]), lambda bank: k_out(a, bank))
+            push(sq, 2, lambda: k_turn(a, prs[a // 4]), lambda bank: k_out(a, bank))
 
         def push_v_out(a):
-            push(sq, SR - 1, lambda: v_bank(a), lambda bank: v_out(a, bank))
+            push(sq, 2, lambda: v_bank(a), lambda bank: v_out(a, bank))
 
 
         prs = [pr0, None]
         gts = [None, None]
-        todo = [lambda a=a: push_k_out(a) for a in range(4)]
 
         def norms_and_table(a):
             return [lambda h=h: push_norm(a, h) for h in range(H)] + [lambda r=r: push_gain(a, r) for r in range(2)]
-        todo += norms_and_table(4) + norms_and_table(5) + norms_and_table(6)
-        todo += [lambda a=a: push_k_norm(a) for a in range(4, 8)]
-        todo += norms_and_table(7)
-        todo += [lambda a=a: push_k_out(a) for a in range(4, 8)]
-        todo += [lambda a=a: push_v_out(a) for a in range(8)]
-        vq.append((q7, lambda bank: do_query(7, bank)))
-        count = 0
-        for n in range(8, NQ):
-            for f in todo[0:2]:
+
+        k_norm = [lambda a=a: push_k_norm(a) for a in range(NT)]
+        ko = [lambda a=a: push_k_out(a) for a in range(NT)]
+        vo = [lambda a=a: push_v_out(a) for a in range(NT)]
+
+        def do(items):
+            for f in items:
                 f()
-            todo = todo[2:]
-            a, h = divmod(n, H)
+
+        vq.append((q7, lambda bank: do_query(7, bank)))
+        for b in range(2, NT):
+            n = H * b
+            if b < 6:
+                nt = norms_and_table(b + 2)
+                groups = [nt[0:2], nt[2:4] + [vo[b - 2]], nt[4:6] + [ko[b - 2]]]
+            else:
+                c = 4 + 2 * (b - 6)
+                groups = [[k_norm[i] for i in range(4, 8)] if b == 6 else [], vo[c : c + 2], ko[c : c + 2]]
             push_query(n)
-            if n == 9:
+            push_query(n + 1)
+            do(groups[0])
+            if b == 2:
                 push_table(3)
-            if n == 8:
                 prs[1] = k_product_tiles()
+                gts[1] = gain_tables(1)
                 for i in range(4):
                     push_k(1, i // 2, i % 2, prs[1])
-                gts[1] = gain_tables(1)
-        for f in todo:
-            f()
+            push_query(n + 2)
+            push_query(n + 3)
+            do(groups[1])
+            do(groups[2])
         settle(sq, 0)
         settle(vq, 0)

@@ -32,7 +32,7 @@ VADD = ()
 SOLO = (NQ - 2, NQ - 1)
 PRB = 2
 T12B = 3
-YB = 5
+YB = 4
 TABB = 4
 
 FLOPS = 2 * T * D * (H * DH + 2 * DH)
@@ -42,7 +42,7 @@ def tile_attention_pa_kernel(tc, x, wq_bytes, wq_scale, wkv, q_norm_w, k_norm_w,
     nc = tc.nc
     with ExitStack() as ctx:
         const = ctx.enter_context(tc.tile_pool(name="const", bufs=1))
-        stage = ctx.enter_context(tc.tile_pool(name="stage", bufs=3))
+        stage = ctx.enter_context(tc.tile_pool(name="stage", bufs=4))
         work = ctx.enter_context(tc.tile_pool(name="work", bufs=3))
         psum = ctx.enter_context(tc.psum_pool(name="psum", bufs=8))
         ctx.enter_context(tc.manual_schedule())
@@ -67,29 +67,30 @@ def tile_attention_pa_kernel(tc, x, wq_bytes, wq_scale, wkv, q_norm_w, k_norm_w,
         scale_row = const.tile([P, D], F32, name="scale_row")
         ident = const.tile([P, P], F32, name="ident")
         trow = [const.tile([P, HT], F32, name="trow%d" % th) for th in range(2)]
+        nc.gpsimd.memset(scale_row[:], 0.0)
+        ones_sq = const.tile([P, P], F32, name="ones_sq")
+        nc.vector.memset(ones_sq[:], 1.0)
         make_identity(nc, ident[:])
-        nc.gpsimd.iota(trow[0][:], pattern=[[1, HT]], base=0, channel_multiplier=0, allow_small_or_imprecise_dtypes=True)
-        gq = const.tile([P, 2, DH], BF16, name="gq")
-        one = const.tile([P, 1], F32, name="one")
-        nc.vector.memset(one[:], 1.0)
-        nc.vector.memset(scale_row[:], 0.0)
-        gain_row = const.tile([P, 2, DH], BF16, name="gain_row")
         sign = const.tile([P, 2], BF16, name="sign")
-        nc.vector.memset(gain_row[:], 0.0)
         nc.vector.memset(sign[:, 0:1], 1.0)
         nc.vector.memset(sign[:, 1:2], -1.0)
+        for th in range(2):
+            nc.gpsimd.iota(trow[th][:], pattern=[[1, HT]], base=HT * th, channel_multiplier=0, allow_small_or_imprecise_dtypes=True)
+        gain_row = const.tile([P, 2, DH], BF16, name="gain_row")
+        nc.gpsimd.memset(gain_row[:].rearrange("p r d -> p (r d)").bitcast(F32), 0.0)
+        gq = const.tile([P, 2, DH], BF16, name="gq")
         gains = const.tile([P, 2, 2, 3], F32, name="gains")
         qg = gains[:, 0]
         kg = gains[:, 1]
         nc.sync.dma_start(out=x_sb[0][:], in_=xv[:, 0:4, :])
-        nc.sync.dma_start(out=scale_row[0:1, :], in_=wq_scale)
+        nc.scalar.dma_start(out=scale_row[0:1, :], in_=wq_scale)
         nc.sync.dma_start(out=wq_b8[0][:], in_=wqv[:, 0:4, :])
         nc.sync.dma_start(out=wkv_sb[0][:], in_=wkvv[:, 0:4, :])
-        nc.sync.dma_start(out=gain_row[0:1, 0, :], in_=q_norm_w.rearrange("(o d) -> o d", o=1))
-        nc.sync.dma_start(out=gain_row[0:1, 1, :], in_=k_norm_w.rearrange("(o d) -> o d", o=1))
         nc.sync.dma_start(out=wq_b8[1][:], in_=wqv[:, 4:8, :])
         nc.sync.dma_start(out=wq_b8[2][:], in_=wqv[:, 8:12, :])
         nc.sync.dma_start(out=wq_b8[3][:], in_=wqv[:, 12:16, :])
+        nc.sync.dma_start(out=gain_row[0:1, 0, :], in_=q_norm_w.rearrange("(o d) -> o d", o=1))
+        nc.sync.dma_start(out=gain_row[0:1, 1, :], in_=k_norm_w.rearrange("(o d) -> o d", o=1))
         nc.sync.dma_start(out=x_sb[1][:], in_=xv[:, 4:8, :])
         nc.sync.dma_start(out=wkv_sb[1][:], in_=wkvv[:, 4:8, :])
         nc.sync.dma_start(out=gq[:, 0, :], in_=q_norm_w.partition_broadcast(P))
@@ -100,21 +101,23 @@ def tile_attention_pa_kernel(tc, x, wq_bytes, wq_scale, wkv, q_norm_w, k_norm_w,
 
         warm = const.tile([P, 2], F32, name="warm")
         grow = const.tile([P, 256], F32, name="grow")
-        nc.scalar.activation(out=grow[:, 0:1], in_=one[:], func=ACT.Copy, scale=1.0 / TWO_PI)
+        nc.scalar.activation(out=warm[:, 0:1], in_=ones_sq[:, 0:1], func=ACT.Sin)
+        nc.vector.tensor_scalar(out=grow[:, 0:1], in0=ones_sq[:, 0:1], scalar1=1.0 / TWO_PI, scalar2=None, op0=ALU.mult)
         for level in range(4):
             w = 4 ** level
             for m in range(1, 4):
-                nc.scalar.activation(
-                    out=grow[:, m * w : (m + 1) * w], in_=grow[:, 0:w], func=ACT.Copy, scale=ROPE_BASE ** (-m * w / 256.0)
+                nc.vector.scalar_tensor_tensor(
+                    out=grow[:, m * w : (m + 1) * w], in0=grow[:, 0:w], scalar=ROPE_BASE ** (-m * w / 256.0), in1=ones_sq[:, 0:w],
+                    op0=ALU.mult, op1=ALU.mult,
                 )
-        nc.scalar.activation(out=warm[:, 0:1], in_=one[:], func=ACT.Sin)
         gps = v_tile([P, 2, P], "gps")
         for j in range(2):
             nc.tensor.transpose(gps[:, j, :], grow[:, P * j : P * (j + 1)], ident[:])
+        spare = v_tile([P, 4, P], "spare")
+        for i in range(12):
+            nc.tensor.transpose(spare[:, i % 4, :], ident[:], ident[:])
         gcol = const.tile([P, 2], F32, name="gcol")
         nc.vector.tensor_copy(out=gcol[:], in_=gps[:, :, 0])
-        ones_sq = const.tile([P, P], F32, name="ones_sq")
-        nc.vector.memset(ones_sq[:], 1.0)
         scale_sb = const.tile([P, D], F32, name="scale_sb")
 
         sinT = [const.tile([P, 2, HT], F32, name="sinT%d" % th) for th in range(2)]
@@ -135,10 +138,8 @@ def tile_attention_pa_kernel(tc, x, wq_bytes, wq_scale, wkv, q_norm_w, k_norm_w,
         def turns_of(th):
             tiles = []
             for j in range(2):
-                turns = stage.tile([P, HT], I32, name="turns", tag="turns", bufs=4)
-                nc.vector.tensor_scalar(
-                    out=turns[:], in0=trow[th][:], scalar1=gcol[:, j : j + 1], scalar2=0.0, op0=ALU.mult, op1=ALU.add
-                )
+                turns = stage.tile([P, HT], U32, name="turns", tag="turns", bufs=2)
+                nc.scalar.activation(out=turns[:], in_=trow[th][:], func=ACT.Copy, scale=gcol[:, j : j + 1])
                 tiles.append(turns)
             return tiles
 
@@ -146,14 +147,17 @@ def tile_attention_pa_kernel(tc, x, wq_bytes, wq_scale, wkv, q_norm_w, k_norm_w,
             frac = stage.tile([P, 2, HT], F32, name="frac", tag="frac", bufs=2)
             for j in range(2):
                 nc.vector.scalar_tensor_tensor(
-                    out=frac[:, j, :], in0=trow[th][:], scalar=gcol[:, j : j + 1], in1=turns[j][:],
+                    out=frac[:, j, :], in0=trow[th][:], scalar=gcol[:, j : j + 1], in1=turns[j][:].bitcast(I32),
                     op0=ALU.mult, op1=ALU.subtract,
                 )
             return frac
 
-        def sin_cos(th, frac):
+        def magnitudes(frac):
             afrac = stage.tile([P, 2, HT], F32, name="afrac", tag="afrac", bufs=1)
             nc.scalar.activation(out=afrac[:], in_=frac[:], func=ACT.Abs)
+            return afrac
+
+        def sin_cos(th, frac, afrac):
             nc.scalar.activation(out=sinT[th][:], in_=frac[:], func=ACT.Sin, scale=TWO_PI)
             nc.scalar.activation(out=cosT[th][:], in_=afrac[:], func=ACT.Sin, scale=-TWO_PI, bias=0.5 * math.pi)
 
@@ -214,7 +218,7 @@ def tile_attention_pa_kernel(tc, x, wq_bytes, wq_scale, wkv, q_norm_w, k_norm_w,
         def widen(h, b):
             wide = []
             for rr in range(2):
-                wqf = stage.tile([P, D], BF16, name="wqf", tag="wqf", bufs=8)
+                wqf = stage.tile([P, D], BF16, name="wqf", tag="wqf", bufs=12)
                 nc.vector.tensor_tensor(out=wqf[:], in0=wq_b8[h][:, 2 * b + rr, :].bitcast(FP8), in1=scale_sb[:], op=ALU.mult)
                 wide.append(wqf)
             return wide
@@ -395,85 +399,86 @@ def tile_attention_pa_kernel(tc, x, wq_bytes, wq_scale, wkv, q_norm_w, k_norm_w,
                 query_out(n - 1, pair[n], 2, n in VADD)
 
         turns0 = turns_of(0)
-        xg0 = x_turn(0, False)
         frac0 = fractions(0, turns0)
         scale_ps = v_tile([P, D], "scale_ps")
         nc.tensor.matmul(out=scale_ps[:], lhsT=ones_sq[:], rhs=scale_row[:], start=True, stop=True)
-        nc.vector.tensor_scalar(out=trow[1][:], in0=trow[0][:], scalar1=float(HT), scalar2=None, op0=ALU.add)
         turns1 = turns_of(1)
-        x_quant(0, xg0)
-        nc.vector.tensor_copy(out=scale_sb[:], in_=scale_ps[:])
-        sin_cos(0, frac0)
-        g0 = wq_turn(wq_widen(0))
+        xg0 = x_turn(0, False)
         frac1 = fractions(1, turns1)
+        nc.vector.tensor_copy(out=scale_sb[:], in_=scale_ps[:])
+        sin_cos(0, frac0, magnitudes(frac0))
+        wide = [wq_widen(0)]
+        x_quant(0, xg0)
         kgrp, kgrpw = group_tile()
         for j, bank in enumerate(wkv_turn(0)):
             exit_split(bank, kgrpw, j)
+        wide.append(wq_widen(1))
+        g0 = wq_turn(wide[0])
         load_gains()
-        g1 = wq_turn(wq_widen(1))
+        wide.append(wq_widen(2))
+        g1 = wq_turn(wide[1])
         quantise(kgrp, wc[4][:], ws[4][:])
-        kb = [k_bank(0, 0, e) for e in range(2)]
         wq_quant(0, g0)
-        sin_cos(1, frac1)
-        nc.scalar.activation(out=warm[:, 1:2], in_=cosT[1][:, 1, HT - 1 : HT], func=ACT.Abs_reciprocal_sqrt, scale=0.0, bias=1.0)
+        kb = [k_bank(0, 0, e) for e in range(2)]
+        wide.append(wq_widen(3))
+        g2 = wq_turn(wide[2])
+        wq_quant(1, g1)
         pr0 = k_product_tiles()
-        tb0 = table_bank(0)
         for i in range(2):
             k_products(0, 0, i, kb[i], pr0)
-        g2 = wq_turn(wq_widen(2))
-        norm(0, 0)
         kb = [k_bank(0, 1, e) for e in range(2)]
-        wq_quant(1, g1)
-        q0 = q_bank(0)
-        g3 = wq_turn(wq_widen(3))
-        norm(0, 1)
+        g3 = wq_turn(wide[3])
+        sin_cos(1, frac1, magnitudes(frac1))
+        nc.scalar.activation(out=warm[:, 1:2], in_=cosT[1][:, 1, HT - 1 : HT], func=ACT.Abs_reciprocal_sqrt, scale=0.0, bias=1.0)
+        tb0 = table_bank(0)
+        wq_quant(2, g2)
+        for i in range(2):
+            k_products(0, 1, i, kb[i], pr0)
+        for h in range(3):
+            norm(0, h)
         gpv = gq[:, 0, :].rearrange("p (i e) -> p i e", e=2)
         gqv = gq[:, 1, :].rearrange("p (i e) -> p i e", e=2)
         nc.vector.tensor_copy(out=gqv[:, :, 0], in_=gpv[:, :, 1])
         nc.vector.tensor_scalar(out=gqv[:, :, 1], in0=gpv[:, :, 0], scalar1=-1.0, scalar2=None, op0=ALU.mult)
-        tabs[0] = table(tb0)
-        wq_quant(2, g2)
-        q1 = q_bank(1)
-        norm(0, 2)
-        xg1 = x_turn(1, False)
-        k_products(0, 1, 0, kb[0], pr0)
         wq_quant(3, g3)
-        q2 = q_bank(2)
+        tabs[0] = table(tb0)
+        xg1 = x_turn(1, True)
         norm(0, 3)
-        k_products(0, 1, 1, kb[1], pr0)
-        x_quant(1, xg1)
-        q3 = q_bank(3)
+        norm_sq(1, 0)
+        norm_sq(1, 1)
         vg, vgw = group_tile()
-        for b, bank in enumerate(wkv_turn(1)):
-            exit_plain(bank, vgw, b, False)
-        do_query(0, q0)
-        tb1 = table_bank(1)
-        for h in range(4):
-            norm_sq(1, h)
+        for b in range(2):
+            exit_plain(turn_pair(wkv_sb[1][:, 2 * b, :], wkv_sb[1][:, 2 * b + 1, :], True), vgw, b, True)
+        norm_sq(1, 2)
+        norm_sq(1, 3)
         inv_rms(inv[1][:], ssq[1][:])
+        q0 = q_bank(0)
+        q1 = q_bank(1)
+        x_quant(1, xg1)
+        quantise(vg, wc[5][:], ws[5][:])
+        do_query(0, q0)
+        q2 = q_bank(2)
+        q3 = q_bank(3)
+        tb1 = table_bank(1)
         do_query(1, q1)
-        q4 = q_bank(4)
-        do_query(2, q2)
-        q5 = q_bank(5)
         for h in range(4):
             norm_sq(2, h)
         inv_rms(inv[2][:], ssq[2][:])
+        do_query(2, q2)
+        q4 = q_bank(4)
         do_query(3, q3)
-        q6 = q_bank(6)
+        q5 = q_bank(5)
         tabs[1] = table(tb1)
-        tb2 = table_bank(2)
-        do_query(4, q4)
-        q7 = q_bank(7)
         for h in range(4):
             norm_sq(3, h)
         inv_rms(inv[3][:], ssq[3][:])
+        tb2 = table_bank(2)
+        q6 = q_bank(6)
+        do_query(4, q4)
+        q7 = q_bank(7)
         do_query(5, q5)
         tabs[2] = table(tb2)
-        quantise(vg, wc[5][:], ws[5][:])
         do_query(6, q6)
-        for a in range(4):
-            square(square_bank(a, H), ssk[:, a : a + 1])
-        inv_rms(invk[:, 0:4], ssk[:, 0:4])
         vq = []
         sq = []
 
@@ -534,31 +539,28 @@ def tile_attention_pa_kernel(tc, x, wq_bytes, wq_scale, wkv, q_norm_w, k_norm_w,
         ko = [lambda a=a: push_k_out(a) for a in range(NT)]
         vo = [lambda a=a: push_v_out(a) for a in range(NT)]
 
-        def do(items):
-            for f in items:
-                f()
-
+        prs[1] = k_product_tiles()
+        gts[1] = gain_tables(1)
+        todo = norms_and_table(4) + k_norm[0:4] + norms_and_table(5) + vo[0:2]
+        todo += norms_and_table(6) + ko[0:2] + vo[2:3] + norms_and_table(7) + ko[2:4] + vo[3:4]
+        todo += k_norm[4:8]
+        for a in range(4, 8):
+            todo += [vo[a], ko[a]]
         vq.append((q7, lambda bank: do_query(7, bank)))
         for b in range(2, NT):
-            n = H * b
-            if b < 6:
-                nt = norms_and_table(b + 2)
-                groups = [nt[0:2], nt[2:4] + [vo[b - 2]], nt[4:6] + [ko[b - 2]]]
-            else:
-                c = 4 + 2 * (b - 6)
-                groups = [[k_norm[i] for i in range(4, 8)] if b == 6 else [], vo[c : c + 2], ko[c : c + 2]]
-            push_query(n)
-            push_query(n + 1)
-            do(groups[0])
-            if b == 2:
-                push_table(3)
-                prs[1] = k_product_tiles()
-                gts[1] = gain_tables(1)
-                for i in range(4):
-                    push_k(1, i // 2, i % 2, prs[1])
-            push_query(n + 2)
-            push_query(n + 3)
-            do(groups[1])
-            do(groups[2])
+            for s in range(2):
+                n = H * b + 2 * s
+                push_query(n)
+                push_query(n + 1)
+                if b == 2 and s == 0:
+                    push_table(3)
+                if 2 <= b < 6 and s == 1:
+                    push_k(1, (b - 2) // 2, b % 2, prs[1])
+                take = 5 if b < 4 else 4
+                for f in todo[0:take]:
+                    f()
+                todo = todo[take:]
+        for f in todo:
+            f()
         settle(sq, 0)
         settle(vq, 0)

@@ -307,7 +307,7 @@ def tile_attention_pa_kernel(tc, x, wq_bytes, wq_scale, wkv, q_norm_w, k_norm_w,
             for r, src in enumerate((cosT[th], sinT[th])):
                 for e in range(2):
                     gt = const.tile([P, 2, HT], F32, name="gt%d%d%d" % (th, r, e), tag="early%d" % (2 * r + e))
-                    gi = e if r == 0 else (1, 2)[e]
+                    gi = e if r == 0 else (2, 1)[e]
                     for j in range(2):
                         nc.scalar.activation(out=gt[:, j, :], in_=src[:, j, :], func=ACT.Copy, scale=qg[:, j, gi : gi + 1])
                     out[r].append(gt)
@@ -348,20 +348,19 @@ def tile_attention_pa_kernel(tc, x, wq_bytes, wq_scale, wkv, q_norm_w, k_norm_w,
 
         def query(n, bank, tab, t12):
             a, h = divmod(n, H)
-            nc.vector.scalar_tensor_tensor(
-                out=t12[:, h % 2], in0=bank[:].unsqueeze(1).to_broadcast([P, 2, DH]), scalar=inv[a][:, h : h + 1],
-                in1=tab[:], op0=ALU.mult, op1=ALU.mult,
-            )
+            for r in range(2):
+                u = bank[:].rearrange("p (i e) -> p i e", e=2)
+                nc.vector.scalar_tensor_tensor(
+                    out=t12[:, h % 2, r, :].rearrange("p (i e) -> p i e", e=2), in0=u if r == 0 else u[:, :, ::-1],
+                    scalar=inv[a][:, h : h + 1], in1=tab[:, r, :].rearrange("p (i e) -> p i e", e=2), op0=ALU.mult, op1=ALU.mult,
+                )
 
         def query_out(n, t12, count, on_vector):
             a, h = divmod(n, H)
             s = h % 2
             y = work.tile([P, 2, DH], F32, name="y", tag="y", bufs=YB)
             (nc.vector if on_vector else nc.gpsimd).tensor_tensor(
-                out=y[:, s : s + count].rearrange("p h (i e) -> p h i e", e=2),
-                in0=t12[:, s : s + count, 0, :].rearrange("p h (i e) -> p h i e", e=2),
-                in1=t12[:, s : s + count, 1, :].rearrange("p h (i e) -> p h i e", e=2)[:, :, :, ::-1],
-                op=ALU.add,
+                out=y[:, s : s + count], in0=t12[:, s : s + count, 0, :], in1=t12[:, s : s + count, 1, :], op=ALU.add,
             )
             nc.sync.dma_start(out=o0v[:, h : h + count, a, :], in_=y[:, s : s + count])
 
@@ -417,6 +416,7 @@ def tile_attention_pa_kernel(tc, x, wq_bytes, wq_scale, wkv, q_norm_w, k_norm_w,
         load_gains()
         wide.append(wq_widen(2))
         g1 = wq_turn(wide[1])
+        sin_cos(1, frac1, magnitudes(frac1))
         quantise(kgrp, wc[4][:], ws[4][:])
         wq_quant(0, g0)
         kb = [k_bank(0, 0, e) for e in range(2)]
@@ -428,7 +428,6 @@ def tile_attention_pa_kernel(tc, x, wq_bytes, wq_scale, wkv, q_norm_w, k_norm_w,
             k_products(0, 0, i, kb[i], pr0)
         kb = [k_bank(0, 1, e) for e in range(2)]
         g3 = wq_turn(wide[3])
-        sin_cos(1, frac1, magnitudes(frac1))
         nc.scalar.activation(out=warm[:, 1:2], in_=cosT[1][:, 1, HT - 1 : HT], func=ACT.Abs_reciprocal_sqrt, scale=0.0, bias=1.0)
         tb0 = table_bank(0)
         wq_quant(2, g2)
@@ -438,8 +437,8 @@ def tile_attention_pa_kernel(tc, x, wq_bytes, wq_scale, wkv, q_norm_w, k_norm_w,
             norm(0, h)
         gpv = gq[:, 0, :].rearrange("p (i e) -> p i e", e=2)
         gqv = gq[:, 1, :].rearrange("p (i e) -> p i e", e=2)
-        nc.vector.tensor_copy(out=gqv[:, :, 0], in_=gpv[:, :, 1])
-        nc.vector.tensor_scalar(out=gqv[:, :, 1], in0=gpv[:, :, 0], scalar1=-1.0, scalar2=None, op0=ALU.mult)
+        nc.vector.tensor_scalar(out=gqv[:, :, 0], in0=gpv[:, :, 0], scalar1=-1.0, scalar2=None, op0=ALU.mult)
+        nc.vector.tensor_copy(out=gqv[:, :, 1], in_=gpv[:, :, 1])
         wq_quant(3, g3)
         tabs[0] = table(tb0)
         xg1 = x_turn(1, True)
@@ -452,6 +451,7 @@ def tile_attention_pa_kernel(tc, x, wq_bytes, wq_scale, wkv, q_norm_w, k_norm_w,
         norm_sq(1, 2)
         norm_sq(1, 3)
         inv_rms(inv[1][:], ssq[1][:])
+        gt1 = gain_tables(1)
         q0 = q_bank(0)
         q1 = q_bank(1)
         x_quant(1, xg1)
@@ -540,7 +540,7 @@ def tile_attention_pa_kernel(tc, x, wq_bytes, wq_scale, wkv, q_norm_w, k_norm_w,
         vo = [lambda a=a: push_v_out(a) for a in range(NT)]
 
         prs[1] = k_product_tiles()
-        gts[1] = gain_tables(1)
+        gts[1] = gt1
         todo = norms_and_table(4) + k_norm[0:4] + norms_and_table(5) + vo[0:2]
         todo += norms_and_table(6) + ko[0:2] + vo[2:3] + norms_and_table(7) + ko[2:4] + vo[3:4]
         todo += k_norm[4:8]

@@ -28,7 +28,7 @@ TWO_PI = 2.0 * math.pi
 
 VR = 4
 SR = 4
-VADD = ()
+VADD = (NQ - 2, NQ - 1)
 SOLO = (NQ - 2, NQ - 1)
 PRB = 2
 T12B = 3
@@ -392,10 +392,12 @@ def tile_attention_pa_kernel(tc, x, wq_bytes, wq_scale, wkv, q_norm_w, k_norm_w,
                 pair[n] = query_pair(n, None)
                 pair[n + 1] = pair[n]
             query(n, bank, tabs[a], pair[n])
-            if n in SOLO:
-                query_out(n, pair[n], 1, n in VADD)
+            if n in VADD:
+                pass
+            elif n in SOLO:
+                query_out(n, pair[n], 1, False)
             elif h % 2 == 1:
-                query_out(n - 1, pair[n], 2, n in VADD)
+                query_out(n - 1, pair[n], 2, False)
 
         turns0 = turns_of(0)
         frac0 = fractions(0, turns0)
@@ -433,15 +435,16 @@ def tile_attention_pa_kernel(tc, x, wq_bytes, wq_scale, wkv, q_norm_w, k_norm_w,
         wq_quant(2, g2)
         for i in range(2):
             k_products(0, 1, i, kb[i], pr0)
-        for h in range(3):
-            norm(0, h)
+        norm(0, 0)
+        norm(0, 1)
+        xg1 = x_turn(1, False)
+        norm(0, 2)
         gpv = gq[:, 0, :].rearrange("p (i e) -> p i e", e=2)
         gqv = gq[:, 1, :].rearrange("p (i e) -> p i e", e=2)
         nc.vector.tensor_scalar(out=gqv[:, :, 0], in0=gpv[:, :, 0], scalar1=-1.0, scalar2=None, op0=ALU.mult)
         nc.vector.tensor_copy(out=gqv[:, :, 1], in_=gpv[:, :, 1])
         wq_quant(3, g3)
         tabs[0] = table(tb0)
-        xg1 = x_turn(1, True)
         norm(0, 3)
         norm_sq(1, 0)
         norm_sq(1, 1)
@@ -541,11 +544,9 @@ def tile_attention_pa_kernel(tc, x, wq_bytes, wq_scale, wkv, q_norm_w, k_norm_w,
 
         prs[1] = k_product_tiles()
         gts[1] = gt1
-        todo = norms_and_table(4) + k_norm[0:4] + norms_and_table(5) + vo[0:2]
-        todo += norms_and_table(6) + ko[0:2] + vo[2:3] + norms_and_table(7) + ko[2:4] + vo[3:4]
-        todo += k_norm[4:8]
-        for a in range(4, 8):
-            todo += [vo[a], ko[a]]
+        todo = norms_and_table(4) + k_norm[0:4] + ko[0:2] + norms_and_table(5) + ko[2:4] + vo[0:2]
+        todo += norms_and_table(6) + vo[2:6] + norms_and_table(7) + k_norm[4:8]
+        todo += vo[6:7] + ko[4:5] + vo[7:8] + ko[5:8]
         vq.append((q7, lambda bank: do_query(7, bank)))
         for b in range(2, NT):
             for s in range(2):
@@ -556,7 +557,7 @@ def tile_attention_pa_kernel(tc, x, wq_bytes, wq_scale, wkv, q_norm_w, k_norm_w,
                     push_table(3)
                 if 2 <= b < 6 and s == 1:
                     push_k(1, (b - 2) // 2, b % 2, prs[1])
-                take = 5 if b < 4 else 4
+                take = 5 if b < 5 else 4
                 for f in todo[0:take]:
                     f()
                 todo = todo[take:]
@@ -564,3 +565,5 @@ def tile_attention_pa_kernel(tc, x, wq_bytes, wq_scale, wkv, q_norm_w, k_norm_w,
             f()
         settle(sq, 0)
         settle(vq, 0)
+        for n in VADD:
+            query_out(n, pair[n], 1, True)

@@ -82,9 +82,9 @@ def tile_attention_pa_kernel(tc, x, wq_bytes, wq_scale, wkv, q_norm_w, k_norm_w,
         gains = const.tile([P, 2, 2, 3], F32, name="gains")
         qg = gains[:, 0]
         kg = gains[:, 1]
-        nc.sync.dma_start(out=x_sb[0][:], in_=xv[:, 0:4, :])
-        nc.scalar.dma_start(out=scale_row[0:1, :], in_=wq_scale)
+        nc.sync.dma_start(out=scale_row[0:1, :], in_=wq_scale)
         nc.sync.dma_start(out=wq_b8[0][:], in_=wqv[:, 0:4, :])
+        nc.sync.dma_start(out=x_sb[0][:], in_=xv[:, 0:4, :])
         nc.sync.dma_start(out=wkv_sb[0][:], in_=wkvv[:, 0:4, :])
         nc.sync.dma_start(out=wq_b8[1][:], in_=wqv[:, 4:8, :])
         nc.sync.dma_start(out=wq_b8[2][:], in_=wqv[:, 8:12, :])
@@ -218,7 +218,7 @@ def tile_attention_pa_kernel(tc, x, wq_bytes, wq_scale, wkv, q_norm_w, k_norm_w,
         def widen(h, b):
             wide = []
             for rr in range(2):
-                wqf = stage.tile([P, D], BF16, name="wqf", tag="wqf", bufs=12)
+                wqf = stage.tile([P, D], BF16, name="wqf", tag="wqf", bufs=10)
                 nc.vector.tensor_tensor(out=wqf[:], in0=wq_b8[h][:, 2 * b + rr, :].bitcast(FP8), in1=scale_sb[:], op=ALU.mult)
                 wide.append(wqf)
             return wide
@@ -226,6 +226,7 @@ def tile_attention_pa_kernel(tc, x, wq_bytes, wq_scale, wkv, q_norm_w, k_norm_w,
         def wkv_turn(c):
             return [turn_pair(wkv_sb[c][:, 2 * b, :], wkv_sb[c][:, 2 * b + 1, :]) for b in range(2)]
 
+        outs = {}
         ssq = []
         inv = []
         for a in range(NT):
@@ -276,12 +277,15 @@ def tile_attention_pa_kernel(tc, x, wq_bytes, wq_scale, wkv, q_norm_w, k_norm_w,
             return yb
 
         def k_out(a, yb):
-            yk = work.tile([P, DH], F32, name="yk", tag="yk", bufs=4)
+            if a % 2 == 0:
+                outs["k"] = work.tile([P, 2, DH], F32, name="yk", tag="yk", bufs=3)
+            yk = outs["k"]
             nc.scalar.activation(
-                out=yk[:].rearrange("p (j i e) -> p j i e", j=2, e=2), in_=yb[:].rearrange("p (j e i) -> p j i e", j=2, e=2),
+                out=yk[:, a % 2, :].rearrange("p (j i e) -> p j i e", j=2, e=2), in_=yb[:].rearrange("p (j e i) -> p j i e", j=2, e=2),
                 func=ACT.Copy, scale=invk[:, a : a + 1],
             )
-            nc.sync.dma_start(out=o1[:, a, :], in_=yk[:])
+            if a % 2 == 1:
+                nc.sync.dma_start(out=o1[:, a - 1 : a + 1, :], in_=yk[:])
 
         def v_bank(a):
             bank = s_tile([P, 512], "vbk")
@@ -290,9 +294,12 @@ def tile_attention_pa_kernel(tc, x, wq_bytes, wq_scale, wkv, q_norm_w, k_norm_w,
             return bank
 
         def v_out(a, bank):
-            vs = work.tile([P, DH], F32, name="vs", tag="vs", bufs=4)
-            nc.scalar.copy(out=vs[:], in_=bank[:])
-            nc.sync.dma_start(out=o2[:, a, :], in_=vs[:])
+            if a % 2 == 0:
+                outs["v"] = work.tile([P, 2, DH], F32, name="vs", tag="vs", bufs=3)
+            vs = outs["v"]
+            nc.scalar.copy(out=vs[:, a % 2, :], in_=bank[:])
+            if a % 2 == 1:
+                nc.sync.dma_start(out=o2[:, a - 1 : a + 1, :], in_=vs[:])
 
         def table_bank(a):
             ps = v_tile([P, 2, 2, P], "tab_ps")
@@ -303,15 +310,13 @@ def tile_attention_pa_kernel(tc, x, wq_bytes, wq_scale, wkv, q_norm_w, k_norm_w,
             return ps
 
         def gain_tables(th):
-            out = [[], []]
-            for r, src in enumerate((cosT[th], sinT[th])):
-                for e in range(2):
-                    gt = const.tile([P, 2, HT], F32, name="gt%d%d%d" % (th, r, e), tag="early%d" % (2 * r + e))
-                    gi = e if r == 0 else (2, 1)[e]
-                    for j in range(2):
-                        nc.scalar.activation(out=gt[:, j, :], in_=src[:, j, :], func=ACT.Copy, scale=qg[:, j, gi : gi + 1])
-                    out[r].append(gt)
-            return out
+            return [[const.tile([P, 2, HT], F32, name="gt%d%d%d" % (th, r, e), tag="early%d" % (2 * r + e)) for e in range(2)] for r in range(2)]
+
+        def gain_table(th, gt, r, e):
+            src = (cosT, sinT)[r][th]
+            gi = e if r == 0 else (2, 1)[e]
+            for j in range(2):
+                nc.scalar.activation(out=gt[r][e][:, j, :], in_=src[:, j, :], func=ACT.Copy, scale=qg[:, j, gi : gi + 1])
 
         def gain_bank(a, r, gt):
             ps = s_tile([P, 2, 2, P], "gtab_ps")
@@ -358,11 +363,15 @@ def tile_attention_pa_kernel(tc, x, wq_bytes, wq_scale, wkv, q_norm_w, k_norm_w,
         def query_out(n, t12, count, on_vector):
             a, h = divmod(n, H)
             s = h % 2
-            y = work.tile([P, 2, DH], F32, name="y", tag="y", bufs=YB)
+            d = 0 if count == 1 else s
+            if count == 1:
+                y = work.tile([P, 1, DH], F32, name="ys", tag="ys", bufs=4)
+            else:
+                y = work.tile([P, 2, DH], F32, name="y", tag="y", bufs=YB)
             (nc.vector if on_vector else nc.gpsimd).tensor_tensor(
-                out=y[:, s : s + count], in0=t12[:, s : s + count, 0, :], in1=t12[:, s : s + count, 1, :], op=ALU.add,
+                out=y[:, d : d + count], in0=t12[:, s : s + count, 0, :], in1=t12[:, s : s + count, 1, :], op=ALU.add,
             )
-            nc.sync.dma_start(out=o0v[:, h : h + count, a, :], in_=y[:, s : s + count])
+            nc.sync.dma_start(out=o0v[:, h : h + count, a, :], in_=y[:, d : d + count])
 
         def wq_widen(h):
             return [widen(h, b) for b in range(2)]
@@ -405,8 +414,8 @@ def tile_attention_pa_kernel(tc, x, wq_bytes, wq_scale, wkv, q_norm_w, k_norm_w,
         nc.tensor.matmul(out=scale_ps[:], lhsT=ones_sq[:], rhs=scale_row[:], start=True, stop=True)
         turns1 = turns_of(1)
         xg0 = x_turn(0, False)
-        frac1 = fractions(1, turns1)
         nc.vector.tensor_copy(out=scale_sb[:], in_=scale_ps[:])
+        frac1 = fractions(1, turns1)
         sin_cos(0, frac0, magnitudes(frac0))
         wide = [wq_widen(0)]
         x_quant(0, xg0)
@@ -445,12 +454,12 @@ def tile_attention_pa_kernel(tc, x, wq_bytes, wq_scale, wkv, q_norm_w, k_norm_w,
         nc.vector.tensor_copy(out=gqv[:, :, 1], in_=gpv[:, :, 1])
         wq_quant(3, g3)
         tabs[0] = table(tb0)
+        vg, vgw = group_tile()
+        for b in range(2):
+            exit_plain(turn_pair(wkv_sb[1][:, 2 * b, :], wkv_sb[1][:, 2 * b + 1, :]), vgw, b, False)
         norm(0, 3)
         norm_sq(1, 0)
         norm_sq(1, 1)
-        vg, vgw = group_tile()
-        for b in range(2):
-            exit_plain(turn_pair(wkv_sb[1][:, 2 * b, :], wkv_sb[1][:, 2 * b + 1, :], True), vgw, b, True)
         norm_sq(1, 2)
         norm_sq(1, 3)
         inv_rms(inv[1][:], ssq[1][:])
@@ -462,19 +471,26 @@ def tile_attention_pa_kernel(tc, x, wq_bytes, wq_scale, wkv, q_norm_w, k_norm_w,
         do_query(0, q0)
         q2 = q_bank(2)
         q3 = q_bank(3)
+        norm_sq(2, 0)
+        norm_sq(2, 1)
         tb1 = table_bank(1)
         do_query(1, q1)
-        for h in range(4):
-            norm_sq(2, h)
+        norm_sq(2, 2)
+        norm_sq(2, 3)
         inv_rms(inv[2][:], ssq[2][:])
+        gain_table(1, gt1, 0, 0)
         do_query(2, q2)
         q4 = q_bank(4)
         do_query(3, q3)
+        norm_sq(3, 0)
+        norm_sq(3, 1)
+        gain_table(1, gt1, 0, 1)
         q5 = q_bank(5)
         tabs[1] = table(tb1)
-        for h in range(4):
-            norm_sq(3, h)
+        norm_sq(3, 2)
+        norm_sq(3, 3)
         inv_rms(inv[3][:], ssq[3][:])
+        gain_table(1, gt1, 1, 0)
         tb2 = table_bank(2)
         q6 = q_bank(6)
         do_query(4, q4)
@@ -482,6 +498,7 @@ def tile_attention_pa_kernel(tc, x, wq_bytes, wq_scale, wkv, q_norm_w, k_norm_w,
         do_query(5, q5)
         tabs[2] = table(tb2)
         do_query(6, q6)
+        gain_table(1, gt1, 1, 1)
         vq = []
         sq = []
 
@@ -546,7 +563,7 @@ def tile_attention_pa_kernel(tc, x, wq_bytes, wq_scale, wkv, q_norm_w, k_norm_w,
         gts[1] = gt1
         todo = norms_and_table(4) + k_norm[0:4] + ko[0:2] + norms_and_table(5) + ko[2:4] + vo[0:2]
         todo += norms_and_table(6) + vo[2:6] + norms_and_table(7) + k_norm[4:8]
-        todo += vo[6:7] + ko[4:5] + vo[7:8] + ko[5:8]
+        todo += vo[6:8] + ko[4:8]
         vq.append((q7, lambda bank: do_query(7, bank)))
         for b in range(2, NT):
             for s in range(2):

@@ -82,8 +82,8 @@ def tile_attention_pa_kernel(tc, x, wq_bytes, wq_scale, wkv, q_norm_w, k_norm_w,
         gains = const.tile([P, 2, 2, 3], F32, name="gains")
         qg = gains[:, 0]
         kg = gains[:, 1]
-        nc.sync.dma_start(out=scale_row[0:1, :], in_=wq_scale)
         nc.sync.dma_start(out=wq_b8[0][:], in_=wqv[:, 0:4, :])
+        nc.sync.dma_start(out=scale_row[0:1, :], in_=wq_scale)
         nc.sync.dma_start(out=x_sb[0][:], in_=xv[:, 0:4, :])
         nc.sync.dma_start(out=wkv_sb[0][:], in_=wkvv[:, 0:4, :])
         nc.sync.dma_start(out=wq_b8[1][:], in_=wqv[:, 4:8, :])

@@ -53,9 +53,9 @@ def tile_attention_pa_kernel(tc, x, wq_bytes, wq_scale, wkv, q_norm_w, k_norm_w,
         def s_tile(shape, name):
             return psum.tile(shape, F32, name=name, tag="sb", bufs=SR)
 
-        xv = x.rearrange("b (r p) k -> p (b r) k", p=P)
-        wqv = wq_bytes.rearrange("(r p) k -> p r k", p=P)
-        wkvv = wkv.rearrange("(r p) k -> p r k", p=P)
+        xv = x.rearrange("b (c p r) k -> p (b c) r k", p=P, r=4)
+        wqv = wq_bytes.rearrange("(c p r) k -> p c r k", p=P, r=4)
+        wkvv = wkv.rearrange("(c p r) k -> p c r k", p=P, r=4)
         x_sb = []
         wkv_sb = []
         wq_b8 = []
@@ -82,17 +82,17 @@ def tile_attention_pa_kernel(tc, x, wq_bytes, wq_scale, wkv, q_norm_w, k_norm_w,
         gains = const.tile([P, 2, 2, 3], F32, name="gains")
         qg = gains[:, 0]
         kg = gains[:, 1]
-        nc.sync.dma_start(out=wq_b8[0][:], in_=wqv[:, 0:4, :])
+        nc.sync.dma_start(out=wq_b8[0][:], in_=wqv[:, 0])
         nc.sync.dma_start(out=scale_row[0:1, :], in_=wq_scale)
-        nc.sync.dma_start(out=x_sb[0][:], in_=xv[:, 0:4, :])
-        nc.sync.dma_start(out=wkv_sb[0][:], in_=wkvv[:, 0:4, :])
-        nc.sync.dma_start(out=wq_b8[1][:], in_=wqv[:, 4:8, :])
-        nc.sync.dma_start(out=wq_b8[2][:], in_=wqv[:, 8:12, :])
-        nc.sync.dma_start(out=wq_b8[3][:], in_=wqv[:, 12:16, :])
+        nc.sync.dma_start(out=x_sb[0][:], in_=xv[:, 0])
+        nc.sync.dma_start(out=wkv_sb[0][:], in_=wkvv[:, 0])
+        nc.sync.dma_start(out=wq_b8[1][:], in_=wqv[:, 1])
+        nc.sync.dma_start(out=wq_b8[2][:], in_=wqv[:, 2])
+        nc.sync.dma_start(out=wq_b8[3][:], in_=wqv[:, 3])
         nc.sync.dma_start(out=gain_row[0:1, 0, :], in_=q_norm_w.rearrange("(o d) -> o d", o=1))
         nc.sync.dma_start(out=gain_row[0:1, 1, :], in_=k_norm_w.rearrange("(o d) -> o d", o=1))
-        nc.sync.dma_start(out=x_sb[1][:], in_=xv[:, 4:8, :])
-        nc.sync.dma_start(out=wkv_sb[1][:], in_=wkvv[:, 4:8, :])
+        nc.sync.dma_start(out=x_sb[1][:], in_=xv[:, 1])
+        nc.sync.dma_start(out=wkv_sb[1][:], in_=wkvv[:, 1])
         nc.sync.dma_start(out=gq[:, 0, :], in_=q_norm_w.partition_broadcast(P))
 
         o0v = out_0.rearrange("b h (a p) d -> p (b h) a d", p=P)
@@ -174,17 +174,17 @@ def tile_attention_pa_kernel(tc, x, wq_bytes, wq_scale, wkv, q_norm_w, k_norm_w,
             return grp, grp[:].bitcast(F32).rearrange("p (n u) -> p n u", u=2)
 
         def exit_plain(bank, grpw, b, on_vector):
-            dst = grpw[:, 256 * b : 256 * (b + 1), :].rearrange("p (r n) u -> p r n u", r=2)
-            src = bank[:].rearrange("p r u n -> p r n u")
+            dst = grpw.rearrange("p (n r) u -> p n r u", r=4)[:, :, 2 * b : 2 * b + 2, :]
+            src = bank[:].rearrange("p r u n -> p n r u")
             if on_vector:
                 nc.vector.tensor_copy(out=dst, in_=src)
             else:
                 nc.scalar.copy(out=dst, in_=src)
 
-        def exit_split(bank, grpw, j):
-            dst = grpw[:, 256 * j : 256 * (j + 1), :].rearrange("p (e r i) u -> p r e i u", e=2, r=2)
-            for rr in range(2):
-                nc.scalar.copy(out=dst[:, rr], in_=bank[:, rr].rearrange("p u (i e) -> p e i u", e=2))
+        def exit_split(bank, grpw, e):
+            dst = grpw.rearrange("p (j e m r) u -> p j e m r u", j=2, e=2, r=2)
+            for j in range(2):
+                nc.scalar.copy(out=dst[:, j, e], in_=bank[:, :, :, 64 * j : 64 * (j + 1)].rearrange("p r u m -> p m r u"))
 
         def quantise(grp, codes, scales):
             nc.vector.quantize_mx(out=codes.bitcast(FP8X4), scales=scales, in_=grp[:])
@@ -413,15 +413,16 @@ def tile_attention_pa_kernel(tc, x, wq_bytes, wq_scale, wkv, q_norm_w, k_norm_w,
         scale_ps = v_tile([P, D], "scale_ps")
         nc.tensor.matmul(out=scale_ps[:], lhsT=ones_sq[:], rhs=scale_row[:], start=True, stop=True)
         turns1 = turns_of(1)
+        afrac0 = magnitudes(frac0)
         xg0 = x_turn(0, False)
         nc.vector.tensor_copy(out=scale_sb[:], in_=scale_ps[:])
         frac1 = fractions(1, turns1)
-        sin_cos(0, frac0, magnitudes(frac0))
+        sin_cos(0, frac0, afrac0)
         wide = [wq_widen(0)]
         x_quant(0, xg0)
         kgrp, kgrpw = group_tile()
-        for j, bank in enumerate(wkv_turn(0)):
-            exit_split(bank, kgrpw, j)
+        for e, bank in enumerate([turn_pair(wkv_sb[0][:, e, :], wkv_sb[0][:, e + 2, :]) for e in range(2)]):
+            exit_split(bank, kgrpw, e)
         wide.append(wq_widen(1))
         g0 = wq_turn(wide[0])
         load_gains()
@@ -458,14 +459,14 @@ def tile_attention_pa_kernel(tc, x, wq_bytes, wq_scale, wkv, q_norm_w, k_norm_w,
         for b in range(2):
             exit_plain(turn_pair(wkv_sb[1][:, 2 * b, :], wkv_sb[1][:, 2 * b + 1, :]), vgw, b, False)
         norm(0, 3)
+        q0 = q_bank(0)
+        q1 = q_bank(1)
         norm_sq(1, 0)
         norm_sq(1, 1)
         norm_sq(1, 2)
         norm_sq(1, 3)
         inv_rms(inv[1][:], ssq[1][:])
         gt1 = gain_tables(1)
-        q0 = q_bank(0)
-        q1 = q_bank(1)
         x_quant(1, xg1)
         quantise(vg, wc[5][:], ws[5][:])
         do_query(0, q0)

@@ -74,8 +74,8 @@ def tile_attention_pa_kernel(tc, x, wq_bytes, wq_scale, wkv, q_norm_w, k_norm_w,
         sign = const.tile([P, 2], BF16, name="sign")
         nc.vector.memset(sign[:, 0:1], 1.0)
         nc.vector.memset(sign[:, 1:2], -1.0)
-        for th in range(2):
-            nc.gpsimd.iota(trow[th][:], pattern=[[1, HT]], base=HT * th, channel_multiplier=0, allow_small_or_imprecise_dtypes=True)
+        nc.gpsimd.iota(trow[0][:, 0 : HT // 2], pattern=[[1, HT // 2]], base=0, channel_multiplier=0, allow_small_or_imprecise_dtypes=True)
+        nc.gpsimd.iota(trow[1][:], pattern=[[1, HT]], base=HT, channel_multiplier=0, allow_small_or_imprecise_dtypes=True)
         gain_row = const.tile([P, 2, DH], BF16, name="gain_row")
         nc.gpsimd.memset(gain_row[:].rearrange("p r d -> p (r d)").bitcast(F32), 0.0)
         gq = const.tile([P, 2, DH], BF16, name="gq")
@@ -100,24 +100,29 @@ def tile_attention_pa_kernel(tc, x, wq_bytes, wq_scale, wkv, q_norm_w, k_norm_w,
         o2 = out_2.rearrange("b (a p) d -> p (b a) d", p=P)
 
         warm = const.tile([P, 2], F32, name="warm")
-        grow = const.tile([P, 256], F32, name="grow")
+        grow = const.tile([P, P], F32, name="grow")
         nc.scalar.activation(out=warm[:, 0:1], in_=ones_sq[:, 0:1], func=ACT.Sin)
         nc.vector.tensor_scalar(out=grow[:, 0:1], in0=ones_sq[:, 0:1], scalar1=1.0 / TWO_PI, scalar2=None, op0=ALU.mult)
-        for level in range(4):
-            w = 4 ** level
-            for m in range(1, 4):
+        for w in (1, 4, 16, 64):
+            for m in range(1, min(4, P // w)):
                 nc.vector.scalar_tensor_tensor(
                     out=grow[:, m * w : (m + 1) * w], in0=grow[:, 0:w], scalar=ROPE_BASE ** (-m * w / 256.0), in1=ones_sq[:, 0:w],
                     op0=ALU.mult, op1=ALU.mult,
                 )
-        gps = v_tile([P, 2, P], "gps")
-        for j in range(2):
-            nc.tensor.transpose(gps[:, j, :], grow[:, P * j : P * (j + 1)], ident[:])
+        gcol = const.tile([P, 2], F32, name="gcol")
+        own = const.tile([P, P], F32, name="own")
+        nc.vector.scalar_tensor_tensor(
+            out=own[:], in0=grow[:], scalar=1.0, in1=ident[:], op0=ALU.mult, op1=ALU.mult, accum_out=gcol[:, 0:1]
+        )
+        nc.vector.tensor_scalar(out=gcol[:, 1:2], in0=gcol[:, 0:1], scalar1=ROPE_BASE ** (-P / 256.0), scalar2=None, op0=ALU.mult)
+        for c in range(2):
+            nc.vector.scalar_tensor_tensor(
+                out=trow[0][:, HT // 2 + P * c : HT // 2 + P * (c + 1)], in0=trow[0][:, P * c : P * (c + 1)], scalar=HT / 2.0,
+                in1=ones_sq[:], op0=ALU.add, op1=ALU.mult,
+            )
         spare = v_tile([P, 4, P], "spare")
         for i in range(12):
             nc.tensor.transpose(spare[:, i % 4, :], ident[:], ident[:])
-        gcol = const.tile([P, 2], F32, name="gcol")
-        nc.vector.tensor_copy(out=gcol[:], in_=gps[:, :, 0])
         scale_sb = const.tile([P, D], F32, name="scale_sb")
 
         sinT = [const.tile([P, 2, HT], F32, name="sinT%d" % th) for th in range(2)]
@@ -138,7 +143,7 @@ def tile_attention_pa_kernel(tc, x, wq_bytes, wq_scale, wkv, q_norm_w, k_norm_w,
         def turns_of(th):
             tiles = []
             for j in range(2):
-                turns = stage.tile([P, HT], U32, name="turns", tag="turns", bufs=2)
+                turns = stage.tile([P, HT], U32, name="turns", tag="turns", bufs=4)
                 nc.scalar.activation(out=turns[:], in_=trow[th][:], func=ACT.Copy, scale=gcol[:, j : j + 1])
                 tiles.append(turns)
             return tiles
@@ -365,7 +370,7 @@ def tile_attention_pa_kernel(tc, x, wq_bytes, wq_scale, wkv, q_norm_w, k_norm_w,
             s = h % 2
             d = 0 if count == 1 else s
             if count == 1:
-                y = work.tile([P, 1, DH], F32, name="ys", tag="ys", bufs=4)
+                y = work.tile([P, 1, DH], F32, name="ys", tag="ys", bufs=2)
             else:
                 y = work.tile([P, 2, DH], F32, name="y", tag="y", bufs=YB)
             (nc.vector if on_vector else nc.gpsimd).tensor_tensor(
@@ -415,8 +420,8 @@ def tile_attention_pa_kernel(tc, x, wq_bytes, wq_scale, wkv, q_norm_w, k_norm_w,
         turns1 = turns_of(1)
         afrac0 = magnitudes(frac0)
         xg0 = x_turn(0, False)
-        nc.vector.tensor_copy(out=scale_sb[:], in_=scale_ps[:])
         frac1 = fractions(1, turns1)
+        nc.vector.tensor_copy(out=scale_sb[:], in_=scale_ps[:])
         sin_cos(0, frac0, afrac0)
         wide = [wq_widen(0)]
         x_quant(0, xg0)

@@ -64,7 +64,7 @@ def tile_attention_pa_kernel(tc, x, wq_bytes, wq_scale, wkv, q_norm_w, k_norm_w,
             wkv_sb.append(const.tile([P, 4, D], BF16, name="wkv_sb%d" % c, tag="early%d" % (2 + c)))
         for c in range(H):
             wq_b8.append(const.tile([P, 4, D], U8, name="wq_b8_%d" % c))
-        scale_row = const.tile([P, D], F32, name="scale_row")
+        scale_row = const.tile([P, P], F32, name="scale_row")
         ident = const.tile([P, P], F32, name="ident")
         trow = [const.tile([P, HT], F32, name="trow%d" % th) for th in range(2)]
         nc.gpsimd.memset(scale_row[:], 0.0)
@@ -74,16 +74,16 @@ def tile_attention_pa_kernel(tc, x, wq_bytes, wq_scale, wkv, q_norm_w, k_norm_w,
         sign = const.tile([P, 2], BF16, name="sign")
         nc.vector.memset(sign[:, 0:1], 1.0)
         nc.vector.memset(sign[:, 1:2], -1.0)
-        nc.gpsimd.iota(trow[0][:, 0 : HT // 2], pattern=[[1, HT // 2]], base=0, channel_multiplier=0, allow_small_or_imprecise_dtypes=True)
-        nc.gpsimd.iota(trow[1][:], pattern=[[1, HT]], base=HT, channel_multiplier=0, allow_small_or_imprecise_dtypes=True)
+        for th in range(2):
+            nc.gpsimd.iota(trow[th][:], pattern=[[1, HT]], base=HT * th, channel_multiplier=0, allow_small_or_imprecise_dtypes=True)
         gain_row = const.tile([P, 2, DH], BF16, name="gain_row")
         nc.gpsimd.memset(gain_row[:].rearrange("p r d -> p (r d)").bitcast(F32), 0.0)
         gq = const.tile([P, 2, DH], BF16, name="gq")
         gains = const.tile([P, 2, 2, 3], F32, name="gains")
         qg = gains[:, 0]
         kg = gains[:, 1]
+        nc.sync.dma_start(out=scale_row[0 : D // P, :], in_=wq_scale.rearrange("o (c n) -> (o c) n", n=P))
         nc.sync.dma_start(out=wq_b8[0][:], in_=wqv[:, 0])
-        nc.sync.dma_start(out=scale_row[0:1, :], in_=wq_scale)
         nc.sync.dma_start(out=x_sb[0][:], in_=xv[:, 0])
         nc.sync.dma_start(out=wkv_sb[0][:], in_=wkvv[:, 0])
         nc.sync.dma_start(out=wq_b8[1][:], in_=wqv[:, 1])
@@ -102,9 +102,12 @@ def tile_attention_pa_kernel(tc, x, wq_bytes, wq_scale, wkv, q_norm_w, k_norm_w,
         warm = const.tile([P, 2], F32, name="warm")
         grow = const.tile([P, P], F32, name="grow")
         nc.scalar.activation(out=warm[:, 0:1], in_=ones_sq[:, 0:1], func=ACT.Sin)
-        nc.vector.tensor_scalar(out=grow[:, 0:1], in0=ones_sq[:, 0:1], scalar1=1.0 / TWO_PI, scalar2=None, op0=ALU.mult)
-        for w in (1, 4, 16, 64):
-            for m in range(1, min(4, P // w)):
+        for m in range(8):
+            nc.vector.tensor_scalar(
+                out=grow[:, m : m + 1], in0=ones_sq[:, 0:1], scalar1=ROPE_BASE ** (-m / 256.0) / TWO_PI, scalar2=None, op0=ALU.mult
+            )
+        for w in (8, 64):
+            for m in range(1, min(8, P // w)):
                 nc.vector.scalar_tensor_tensor(
                     out=grow[:, m * w : (m + 1) * w], in0=grow[:, 0:w], scalar=ROPE_BASE ** (-m * w / 256.0), in1=ones_sq[:, 0:w],
                     op0=ALU.mult, op1=ALU.mult,
@@ -115,11 +118,6 @@ def tile_attention_pa_kernel(tc, x, wq_bytes, wq_scale, wkv, q_norm_w, k_norm_w,
             out=own[:], in0=grow[:], scalar=1.0, in1=ident[:], op0=ALU.mult, op1=ALU.mult, accum_out=gcol[:, 0:1]
         )
         nc.vector.tensor_scalar(out=gcol[:, 1:2], in0=gcol[:, 0:1], scalar1=ROPE_BASE ** (-P / 256.0), scalar2=None, op0=ALU.mult)
-        for c in range(2):
-            nc.vector.scalar_tensor_tensor(
-                out=trow[0][:, HT // 2 + P * c : HT // 2 + P * (c + 1)], in0=trow[0][:, P * c : P * (c + 1)], scalar=HT / 2.0,
-                in1=ones_sq[:], op0=ALU.add, op1=ALU.mult,
-            )
         spare = v_tile([P, 4, P], "spare")
         for i in range(12):
             nc.tensor.transpose(spare[:, i % 4, :], ident[:], ident[:])
@@ -416,7 +414,10 @@ def tile_attention_pa_kernel(tc, x, wq_bytes, wq_scale, wkv, q_norm_w, k_norm_w,
         turns0 = turns_of(0)
         frac0 = fractions(0, turns0)
         scale_ps = v_tile([P, D], "scale_ps")
-        nc.tensor.matmul(out=scale_ps[:], lhsT=ones_sq[:], rhs=scale_row[:], start=True, stop=True)
+        for c in range(D // P):
+            nc.tensor.matmul(
+                out=scale_ps[:, P * c : P * (c + 1)], lhsT=ident[:, c : c + 1].to_broadcast([P, P]), rhs=scale_row[:], start=True, stop=True
+            )
         turns1 = turns_of(1)
         afrac0 = magnitudes(frac0)
         xg0 = x_turn(0, False)

from contextlib import ExitStack
import math

import concourse.mybir as mybir
from concourse.masks import make_identity

F32 = mybir.dt.float32
BF16 = mybir.dt.bfloat16
I32 = mybir.dt.int32
U32 = mybir.dt.uint32
U8 = mybir.dt.uint8
FP8 = mybir.dt.float8_e4m3fn
FP8X4 = mybir.dt.float8_e4m3fn_x4
ALU = mybir.AluOpType
ACT = mybir.ActivationFunctionType

P = 128
T = 1024
HT = T // 2
D = 512
DH = 512
H = 4
NT = T // P
NQ = NT * H
ROPE_BASE = 10000.0
EPS = 1.1920929e-07
TWO_PI = 2.0 * math.pi

VR = 4
SR = 4
VADD = (NQ - 2, NQ - 1)
SOLO = (NQ - 2, NQ - 1)
PRB = 2
T12B = 3
YB = 4
TABB = 4

FLOPS = 2 * T * D * (H * DH + 2 * DH)


def tile_attention_pa_kernel(tc, x, wq_bytes, wq_scale, wkv, q_norm_w, k_norm_w, out_0, out_1, out_2):
    nc = tc.nc
    with ExitStack() as ctx:
        const = ctx.enter_context(tc.tile_pool(name="const", bufs=1))
        stage = ctx.enter_context(tc.tile_pool(name="stage", bufs=4))
        work = ctx.enter_context(tc.tile_pool(name="work", bufs=3))
        psum = ctx.enter_context(tc.psum_pool(name="psum", bufs=8))
        ctx.enter_context(tc.manual_schedule())

        def v_tile(shape, name):
            return psum.tile(shape, F32, name=name, tag="vb", bufs=VR)

        def s_tile(shape, name):
            return psum.tile(shape, F32, name=name, tag="sb", bufs=SR)

        xv = x.rearrange("b (c p r) k -> p (b c) r k", p=P, r=4)
        wqv = wq_bytes.rearrange("(c p r) k -> p c r k", p=P, r=4)
        wkvv = wkv.rearrange("(c p r) k -> p c r k", p=P, r=4)
        x_sb = []
        wkv_sb = []
        wq_b8 = []
        for c in range(2):
            x_sb.append(const.tile([P, 4, D], BF16, name="x_sb%d" % c, tag="early%d" % c))
            wkv_sb.append(const.tile([P, 4, D], BF16, name="wkv_sb%d" % c, tag="early%d" % (2 + c)))
        for c in range(H):
            wq_b8.append(const.tile([P, 4, D], U8, name="wq_b8_%d" % c))
        scale_row = const.tile([P, P], F32, name="scale_row")
        ident = const.tile([P, P], F32, name="ident")
        trow = [const.tile([P, HT], F32, name="trow%d" % th) for th in range(2)]
        nc.gpsimd.memset(scale_row[:], 0.0)
        ones_sq = const.tile([P, P], F32, name="ones_sq")
        nc.vector.memset(ones_sq[:], 1.0)
        make_identity(nc, ident[:])
        sign = const.tile([P, 2], BF16, name="sign")
        nc.vector.memset(sign[:, 0:1], 1.0)
        nc.vector.memset(sign[:, 1:2], -1.0)
        for th in range(2):
            nc.gpsimd.iota(trow[th][:], pattern=[[1, HT]], base=HT * th, channel_multiplier=0, allow_small_or_imprecise_dtypes=True)
        gain_row = const.tile([P, 2, DH], BF16, name="gain_row")
        nc.gpsimd.memset(gain_row[:].rearrange("p r d -> p (r d)").bitcast(F32), 0.0)
        gq = const.tile([P, 2, DH], BF16, name="gq")
        gains = const.tile([P, 2, 2, 3], F32, name="gains")
        qg = gains[:, 0]
        kg = gains[:, 1]
        nc.sync.dma_start(out=scale_row[0 : D // P, :], in_=wq_scale.rearrange("o (c n) -> (o c) n", n=P))
        nc.sync.dma_start(out=wq_b8[0][:], in_=wqv[:, 0])
        nc.sync.dma_start(out=x_sb[0][:], in_=xv[:, 0])
        nc.sync.dma_start(out=wkv_sb[0][:], in_=wkvv[:, 0])
        nc.sync.dma_start(out=wq_b8[1][:], in_=wqv[:, 1])
        nc.sync.dma_start(out=wq_b8[2][:], in_=wqv[:, 2])
        nc.sync.dma_start(out=wq_b8[3][:], in_=wqv[:, 3])
        nc.sync.dma_start(out=gain_row[0:1, 0, :], in_=q_norm_w.rearrange("(o d) -> o d", o=1))
        nc.sync.dma_start(out=gain_row[0:1, 1, :], in_=k_norm_w.rearrange("(o d) -> o d", o=1))
        nc.sync.dma_start(out=x_sb[1][:], in_=xv[:, 1])
        nc.sync.dma_start(out=wkv_sb[1][:], in_=wkvv[:, 1])
        nc.sync.dma_start(out=gq[:, 0, :], in_=q_norm_w.partition_broadcast(P))

        o0v = out_0.rearrange("b h (a p) d -> p (b h) a d", p=P)
        o1 = out_1.rearrange("b (a p) d -> p (b a) d", p=P)
        o2 = out_2.rearrange("b (a p) d -> p (b a) d", p=P)

        warm = const.tile([P, 2], F32, name="warm")
        grow = const.tile([P, P], F32, name="grow")
        nc.scalar.activation(out=warm[:, 0:1], in_=ones_sq[:, 0:1], func=ACT.Sin)
        for m in range(8):
            nc.vector.tensor_scalar(
                out=grow[:, m : m + 1], in0=ones_sq[:, 0:1], scalar1=ROPE_BASE ** (-m / 256.0) / TWO_PI, scalar2=None, op0=ALU.mult
            )
        for w in (8, 64):
            for m in range(1, min(8, P // w)):
                nc.vector.scalar_tensor_tensor(
                    out=grow[:, m * w : (m + 1) * w], in0=grow[:, 0:w], scalar=ROPE_BASE ** (-m * w / 256.0), in1=ones_sq[:, 0:w],
                    op0=ALU.mult, op1=ALU.mult,
                )
        gcol = const.tile([P, 2], F32, name="gcol")
        own = const.tile([P, P], F32, name="own")
        nc.vector.scalar_tensor_tensor(
            out=own[:], in0=grow[:], scalar=1.0, in1=ident[:], op0=ALU.mult, op1=ALU.mult, accum_out=gcol[:, 0:1]
        )
        nc.vector.tensor_scalar(out=gcol[:, 1:2], in0=gcol[:, 0:1], scalar1=ROPE_BASE ** (-P / 256.0), scalar2=None, op0=ALU.mult)
        spare = v_tile([P, 4, P], "spare")
        for i in range(12):
            nc.tensor.transpose(spare[:, i % 4, :], ident[:], ident[:])
        scale_sb = const.tile([P, D], F32, name="scale_sb")

        sinT = [const.tile([P, 2, HT], F32, name="sinT%d" % th) for th in range(2)]
        cosT = [const.tile([P, 2, HT], F32, name="cosT%d" % th) for th in range(2)]
        half = [slice(0, HT), slice(HT, T)]

        def load_gains():
            ps = s_tile([P, 2, 2, 3], "gain_ps")
            for r in range(2):
                for j in range(2):
                    for c, (e, s) in enumerate(((0, 0), (1, 0), (0, 1))):
                        nc.tensor.matmul(
                            out=ps[:, r, j, c : c + 1], lhsT=gain_row[:, r, 256 * j + e : 256 * (j + 1) : 2], rhs=sign[:, s : s + 1],
                            start=True, stop=True,
                        )
            nc.scalar.copy(out=gains[:], in_=ps[:])

        def turns_of(th):
            tiles = []
            for j in range(2):
                turns = stage.tile([P, HT], U32, name="turns", tag="turns", bufs=4)
                nc.scalar.activation(out=turns[:], in_=trow[th][:], func=ACT.Copy, scale=gcol[:, j : j + 1])
                tiles.append(turns)
            return tiles

        def fractions(th, turns):
            frac = stage.tile([P, 2, HT], F32, name="frac", tag="frac", bufs=2)
            for j in range(2):
                nc.vector.scalar_tensor_tensor(
                    out=frac[:, j, :], in0=trow[th][:], scalar=gcol[:, j : j + 1], in1=turns[j][:].bitcast(I32),
                    op0=ALU.mult, op1=ALU.subtract,
                )
            return frac

        def magnitudes(frac):
            afrac = stage.tile([P, 2, HT], F32, name="afrac", tag="afrac", bufs=1)
            nc.scalar.activation(out=afrac[:], in_=frac[:], func=ACT.Abs)
            return afrac

        def sin_cos(th, frac, afrac):
            nc.scalar.activation(out=sinT[th][:], in_=frac[:], func=ACT.Sin, scale=TWO_PI)
            nc.scalar.activation(out=cosT[th][:], in_=afrac[:], func=ACT.Sin, scale=-TWO_PI, bias=0.5 * math.pi)

        def turn_pair(rows0, rows1, on_vector=False):
            bank = (v_tile if on_vector else s_tile)([P, 2, 2, P], "tbank")
            for rr, rows in enumerate((rows0, rows1)):
                words = rows.bitcast(F32)
                for u in range(2):
                    nc.tensor.transpose(bank[:, rr, u, :], words[:, u : D // 2 : 2], ident[:])
            return bank

        def group_tile():
            grp = stage.tile([P, 4 * 512], BF16, name="grp", tag="grp", align_bytes=64)
            return grp, grp[:].bitcast(F32).rearrange("p (n u) -> p n u", u=2)

        def exit_plain(bank, grpw, b, on_vector):
            dst = grpw.rearrange("p (n r) u -> p n r u", r=4)[:, :, 2 * b : 2 * b + 2, :]
            src = bank[:].rearrange("p r u n -> p n r u")
            if on_vector:
                nc.vector.tensor_copy(out=dst, in_=src)
            else:
                nc.scalar.copy(out=dst, in_=src)

        def exit_split(bank, grpw, e):
            dst = grpw.rearrange("p (j e m r) u -> p j e m r u", j=2, e=2, r=2)
            for j in range(2):
                nc.scalar.copy(out=dst[:, j, e], in_=bank[:, :, :, 64 * j : 64 * (j + 1)].rearrange("p r u m -> p m r u"))

        def quantise(grp, codes, scales):
            nc.vector.quantize_mx(out=codes.bitcast(FP8X4), scales=scales, in_=grp[:])

        xc = const.tile([P, T], U32, name="xc", align_bytes=64)
        xs = const.tile([P, T], U8, name="xs", align_bytes=64)
        wc = []
        ws = []
        for g in range(6):
            wc.append(const.tile([P, 512], U32, name="wc%d" % g, align_bytes=64))
            ws.append(const.tile([P, 512], U8, name="ws%d" % g, align_bytes=64))

        def mx(out, lc, ls, rc, rs):
            nc.tensor.matmul_mx(
                out=out, lhsT=lc.bitcast(FP8X4), lhsT_scale=ls, rhs=rc.bitcast(FP8X4), rhs_scale=rs, start=True, stop=True
            )

        def x_cols(a):
            return xc[:, P * a : P * (a + 1)], xs[:, P * a : P * (a + 1)]

        def x_turn(c, on_vector):
            grp, grpw = group_tile()
            banks = [turn_pair(x_sb[c][:, 2 * b, :], x_sb[c][:, 2 * b + 1, :], on_vector) for b in range(2)]
            for b in range(2):
                exit_plain(banks[b], grpw, b, on_vector)
            return grp

        def x_quant(c, grp):
            quantise(grp, xc[:, 512 * c : 512 * (c + 1)], xs[:, 512 * c : 512 * (c + 1)])

        def widen(h, b):
            wide = []
            for rr in range(2):
                wqf = stage.tile([P, D], BF16, name="wqf", tag="wqf", bufs=10)
                nc.vector.tensor_tensor(out=wqf[:], in0=wq_b8[h][:, 2 * b + rr, :].bitcast(FP8), in1=scale_sb[:], op=ALU.mult)
                wide.append(wqf)
            return wide

        def wkv_turn(c):
            return [turn_pair(wkv_sb[c][:, 2 * b, :], wkv_sb[c][:, 2 * b + 1, :]) for b in range(2)]

        outs = {}
        ssq = []
        inv = []
        for a in range(NT):
            ssq.append(const.tile([P, H], F32, name="ssq%d" % a))
            inv.append(const.tile([P, H], F32, name="inv%d" % a))
        ssk = const.tile([P, NT], F32, name="ssk")
        invk = const.tile([P, NT], F32, name="invk")

        def square_bank(a, g):
            bank = s_tile([P, 512], "sq")
            lc, ls = x_cols(a)
            mx(bank[:], lc, ls, wc[g][:], ws[g][:])
            return bank

        def square(bank, acc):
            junk = stage.tile([P, 512], BF16, name="junk", tag="junk", bufs=2)
            nc.scalar.activation(out=junk[:], in_=bank[:], func=ACT.Square, accum_out=acc)

        def inv_rms(out, ss):
            nc.scalar.activation(out=out, in_=ss, func=ACT.Abs_reciprocal_sqrt, scale=1.0 / DH, bias=EPS)

        def k_bank(th, j, e):
            u = v_tile([P, 512], "ukt")
            csl = slice(256 * j + P * e, 256 * j + P * (e + 1))
            mx(u[:], wc[4][:, csl], ws[4][:, csl], xc[:, half[th]], xs[:, half[th]])
            return u

        def k_product_tiles():
            return [work.tile([P, 2, 512], F32, name="pr%d" % q, tag="pr%d" % q, bufs=PRB) for q in range(4)]

        def k_products(th, j, e, u, pr):
            for q, gi, tab in (((0, 0, cosT), (2, 1, sinT)), ((1, 2, sinT), (3, 1, cosT)))[e]:
                nc.vector.scalar_tensor_tensor(
                    out=pr[q][:, j, :], in0=u[:], scalar=kg[:, j, gi : gi + 1], in1=tab[th][:, j, :],
                    op0=ALU.mult, op1=ALU.mult,
                )

        def k_turn(a, pr):
            yb = s_tile([P, 512], "ykb")
            tb = a % 4
            for j in range(2):
                for e in range(2):
                    for m in range(2):
                        nc.tensor.matmul(
                            out=yb[:, 256 * j + P * e : 256 * j + P * (e + 1)], lhsT=pr[2 * e + m][:, j, P * tb : P * (tb + 1)],
                            rhs=ident[:], is_transpose=True, start=(m == 0), stop=(m == 1),
                        )
            return yb

        def k_out(a, yb):
            if a % 2 == 0:
                outs["k"] = work.tile([P, 2, DH], F32, name="yk", tag="yk", bufs=3)
            yk = outs["k"]
            nc.scalar.activation(
                out=yk[:, a % 2, :].rearrange("p (j i e) -> p j i e", j=2, e=2), in_=yb[:].rearrange("p (j e i) -> p j i e", j=2, e=2),
                func=ACT.Copy, scale=invk[:, a : a + 1],
            )
            if a % 2 == 1:
                nc.sync.dma_start(out=o1[:, a - 1 : a + 1, :], in_=yk[:])

        def v_bank(a):
            bank = s_tile([P, 512], "vbk")
            lc, ls = x_cols(a)
            mx(bank[:], lc, ls, wc[5][:], ws[5][:])
            return bank

        def v_out(a, bank):
            if a % 2 == 0:
                outs["v"] = work.tile([P, 2, DH], F32, name="vs", tag="vs", bufs=3)
            vs = outs["v"]
            nc.scalar.copy(out=vs[:, a % 2, :], in_=bank[:])
            if a % 2 == 1:
                nc.sync.dma_start(out=o2[:, a - 1 : a + 1, :], in_=vs[:])

        def table_bank(a):
            ps = v_tile([P, 2, 2, P], "tab_ps")
            th, c = divmod(a, 4)
            for r, src in enumerate((cosT[th], sinT[th])):
                for j in range(2):
                    nc.tensor.transpose(ps[:, r, j, :], src[:, j, P * c : P * (c + 1)], ident[:])
            return ps

        def gain_tables(th):
            return [[const.tile([P, 2, HT], F32, name="gt%d%d%d" % (th, r, e), tag="early%d" % (2 * r + e)) for e in range(2)] for r in range(2)]

        def gain_table(th, gt, r, e):
            src = (cosT, sinT)[r][th]
            gi = e if r == 0 else (2, 1)[e]
            for j in range(2):
                nc.scalar.activation(out=gt[r][e][:, j, :], in_=src[:, j, :], func=ACT.Copy, scale=qg[:, j, gi : gi + 1])

        def gain_bank(a, r, gt):
            ps = s_tile([P, 2, 2, P], "gtab_ps")
            c = a % 4
            for e in range(2):
                for j in range(2):
                    nc.tensor.transpose(ps[:, e, j, :], gt[r][e][:, j, P * c : P * (c + 1)], ident[:])
            return ps

        def gain_out(ps, tab, r):
            nc.scalar.copy(
                out=tab[:, r, :].rearrange("p (j i e) -> p j i e", j=2, e=2), in_=ps[:].rearrange("p e j i -> p j i e")
            )

        def table(ps):
            tab = work.tile([P, 2, DH], F32, name="tab", tag="tab", bufs=TABB)
            nc.vector.tensor_tensor(
                out=tab[:].rearrange("p r (i e) -> p (r i) e", e=2),
                in0=ps[:].rearrange("p r j i -> p (r j i)").unsqueeze(2).to_broadcast([P, DH, 2]),
                in1=gq[:].rearrange("p r (i e) -> p (r i) e", e=2),
                op=ALU.mult,
            )
            return tab

        def q_bank(n):
            a, h = divmod(n, H)
            bank = v_tile([P, 512], "qb")
            lc, ls = x_cols(a)
            mx(bank[:], lc, ls, wc[h][:], ws[h][:])
            return bank

        def query_pair(n, tab):
            return work.tile([P, 2, 2, DH], F32, name="t12", tag="t12", bufs=T12B)

        def query(n, bank, tab, t12):
            a, h = divmod(n, H)
            for r in range(2):
                u = bank[:].rearrange("p (i e) -> p i e", e=2)
                nc.vector.scalar_tensor_tensor(
                    out=t12[:, h % 2, r, :].rearrange("p (i e) -> p i e", e=2), in0=u if r == 0 else u[:, :, ::-1],
                    scalar=inv[a][:, h : h + 1], in1=tab[:, r, :].rearrange("p (i e) -> p i e", e=2), op0=ALU.mult, op1=ALU.mult,
                )

        def query_out(n, t12, count, on_vector):
            a, h = divmod(n, H)
            s = h % 2
            d = 0 if count == 1 else s
            if count == 1:
                y = work.tile([P, 1, DH], F32, name="ys", tag="ys", bufs=2)
            else:
                y = work.tile([P, 2, DH], F32, name="y", tag="y", bufs=YB)
            (nc.vector if on_vector else nc.gpsimd).tensor_tensor(
                out=y[:, d : d + count], in0=t12[:, s : s + count, 0, :], in1=t12[:, s : s + count, 1, :], op=ALU.add,
            )
            nc.sync.dma_start(out=o0v[:, h : h + count, a, :], in_=y[:, d : d + count])

        def wq_widen(h):
            return [widen(h, b) for b in range(2)]

        def wq_turn(wide, on_vector=False):
            grp, grpw = group_tile()
            for b in range(2):
                exit_plain(turn_pair(wide[b][0][:], wide[b][1][:], on_vector), grpw, b, on_vector)
            return grp

        def wq_quant(h, grp):
            quantise(grp, wc[h][:], ws[h][:])

        def norm_sq(a, h):
            square(square_bank(a, h), ssq[a][:, h : h + 1])

        def norm(a, h):
            square(square_bank(a, h), ssq[a][:, h : h + 1])
            inv_rms(inv[a][:, h : h + 1], ssq[a][:, h : h + 1])

        tabs = {}
        pair = {}

        def do_query(n, bank):
            a, h = divmod(n, H)
            if n not in pair:
                pair[n] = query_pair(n, None)
                pair[n + 1] = pair[n]
            query(n, bank, tabs[a], pair[n])
            if n in VADD:
                pass
            elif n in SOLO:
                query_out(n, pair[n], 1, False)
            elif h % 2 == 1:
                query_out(n - 1, pair[n], 2, False)

        turns0 = turns_of(0)
        frac0 = fractions(0, turns0)
        scale_ps = v_tile([P, D], "scale_ps")
        for c in range(D // P):
            nc.tensor.matmul(
                out=scale_ps[:, P * c : P * (c + 1)], lhsT=ident[:, c : c + 1].to_broadcast([P, P]), rhs=scale_row[:], start=True, stop=True
            )
        turns1 = turns_of(1)
        afrac0 = magnitudes(frac0)
        xg0 = x_turn(0, False)
        frac1 = fractions(1, turns1)
        nc.vector.tensor_copy(out=scale_sb[:], in_=scale_ps[:])
        sin_cos(0, frac0, afrac0)
        wide = [wq_widen(0)]
        x_quant(0, xg0)
        kgrp, kgrpw = group_tile()
        for e, bank in enumerate([turn_pair(wkv_sb[0][:, e, :], wkv_sb[0][:, e + 2, :]) for e in range(2)]):
            exit_split(bank, kgrpw, e)
        wide.append(wq_widen(1))
        g0 = wq_turn(wide[0])
        load_gains()
        wide.append(wq_widen(2))
        g1 = wq_turn(wide[1])
        sin_cos(1, frac1, magnitudes(frac1))
        quantise(kgrp, wc[4][:], ws[4][:])
        wq_quant(0, g0)
        kb = [k_bank(0, 0, e) for e in range(2)]
        wide.append(wq_widen(3))
        g2 = wq_turn(wide[2])
        wq_quant(1, g1)
        pr0 = k_product_tiles()
        for i in range(2):
            k_products(0, 0, i, kb[i], pr0)
        kb = [k_bank(0, 1, e) for e in range(2)]
        g3 = wq_turn(wide[3])
        nc.scalar.activation(out=warm[:, 1:2], in_=cosT[1][:, 1, HT - 1 : HT], func=ACT.Abs_reciprocal_sqrt, scale=0.0, bias=1.0)
        tb0 = table_bank(0)
        wq_quant(2, g2)
        for i in range(2):
            k_products(0, 1, i, kb[i], pr0)
        norm(0, 0)
        norm(0, 1)
        xg1 = x_turn(1, False)
        norm(0, 2)
        gpv = gq[:, 0, :].rearrange("p (i e) -> p i e", e=2)
        gqv = gq[:, 1, :].rearrange("p (i e) -> p i e", e=2)
        nc.vector.tensor_scalar(out=gqv[:, :, 0], in0=gpv[:, :, 0], scalar1=-1.0, scalar2=None, op0=ALU.mult)
        nc.vector.tensor_copy(out=gqv[:, :, 1], in_=gpv[:, :, 1])
        wq_quant(3, g3)
        tabs[0] = table(tb0)
        vg, vgw = group_tile()
        for b in range(2):
            exit_plain(turn_pair(wkv_sb[1][:, 2 * b, :], wkv_sb[1][:, 2 * b + 1, :]), vgw, b, False)
        norm(0, 3)
        q0 = q_bank(0)
        q1 = q_bank(1)
        norm_sq(1, 0)
        norm_sq(1, 1)
        norm_sq(1, 2)
        norm_sq(1, 3)
        inv_rms(inv[1][:], ssq[1][:])
        gt1 = gain_tables(1)
        x_quant(1, xg1)
        quantise(vg, wc[5][:], ws[5][:])
        do_query(0, q0)
        q2 = q_bank(2)
        q3 = q_bank(3)
        norm_sq(2, 0)
        norm_sq(2, 1)
        tb1 = table_bank(1)
        do_query(1, q1)
        norm_sq(2, 2)
        norm_sq(2, 3)
        inv_rms(inv[2][:], ssq[2][:])
        gain_table(1, gt1, 0, 0)
        do_query(2, q2)
        q4 = q_bank(4)
        do_query(3, q3)
        norm_sq(3, 0)
        norm_sq(3, 1)
        gain_table(1, gt1, 0, 1)
        q5 = q_bank(5)
        tabs[1] = table(tb1)
        norm_sq(3, 2)
        norm_sq(3, 3)
        inv_rms(inv[3][:], ssq[3][:])
        gain_table(1, gt1, 1, 0)
        tb2 = table_bank(2)
        q6 = q_bank(6)
        do_query(4, q4)
        q7 = q_bank(7)
        do_query(5, q5)
        tabs[2] = table(tb2)
        do_query(6, q6)
        gain_table(1, gt1, 1, 1)
        vq = []
        sq = []

        def push(stream, look, fill, drain):
            stream.append((fill(), drain))
            settle(stream, look)

        def settle(stream, look):
            while len(stream) > look:
                bank, drain = stream[0]
                stream.remove(stream[0])
                drain(bank)

        def push_query(n):
            push(vq, 3, lambda: q_bank(n), lambda bank: do_query(n, bank))

        def push_table(a):
            def drain(bank):
                tabs[a] = table(bank)
            push(vq, 3, lambda: table_bank(a), drain)

        def push_gain(a, r):
            if r == 0:
                tabs[a] = work.tile([P, 2, DH], F32, name="tab", tag="tab", bufs=TABB)
            push(sq, 2, lambda: gain_bank(a, r, gts[a // 4]), lambda bank: gain_out(bank, tabs[a], r))

        def push_k(th, j, e, pr):
            push(vq, 3, lambda: k_bank(th, j, e), lambda bank: k_products(th, j, e, bank, pr))

        def push_norm(a, h):
            def drain(bank):
                square(bank, ssq[a][:, h : h + 1])
                if h == H - 1:
                    inv_rms(inv[a][:], ssq[a][:])
            push(sq, 2, lambda: square_bank(a, h), drain)

        def push_k_norm(a):
            def drain(bank):
                square(bank, ssk[:, a : a + 1])
                if a % 4 == 3:
                    inv_rms(invk[:, a - 3 : a + 1], ssk[:, a - 3 : a + 1])
            push(sq, 2, lambda: square_bank(a, H), drain)

        def push_k_out(a):
            push(sq, 2, lambda: k_turn(a, prs[a // 4]), lambda bank: k_out(a, bank))

        def push_v_out(a):
            push(sq, 2, lambda: v_bank(a), lambda bank: v_out(a, bank))


        prs = [pr0, None]
        gts = [None, None]

        def norms_and_table(a):
            return [lambda h=h: push_norm(a, h) for h in range(H)] + [lambda r=r: push_gain(a, r) for r in range(2)]

        k_norm = [lambda a=a: push_k_norm(a) for a in range(NT)]
        ko = [lambda a=a: push_k_out(a) for a in range(NT)]
        vo = [lambda a=a: push_v_out(a) for a in range(NT)]

        prs[1] = k_product_tiles()
        gts[1] = gt1
        todo = norms_and_table(4) + k_norm[0:4] + ko[0:2] + norms_and_table(5) + ko[2:4] + vo[0:2]
        todo += norms_and_table(6) + vo[2:6] + norms_and_table(7) + k_norm[4:8]
        todo += vo[6:8] + ko[4:8]
        vq.append((q7, lambda bank: do_query(7, bank)))
        for b in range(2, NT):
            for s in range(2):
                n = H * b + 2 * s
                push_query(n)
                push_query(n + 1)
                if b == 2 and s == 0:
                    push_table(3)
                if 2 <= b < 6 and s == 1:
                    push_k(1, (b - 2) // 2, b % 2, prs[1])
                take = 5 if b < 5 else 4
                for f in todo[0:take]:
                    f()
                todo = todo[take:]
        for f in todo:
            f()
        settle(sq, 0)
        settle(vq, 0)
        for n in VADD:
            query_out(n, pair[n], 1, True)
